import numpy as np
import ml_dtypes


def mxq(x, axis, fmt="e4m3"):
    dtype, down = {"e4m3": (ml_dtypes.float8_e4m3fn, 7), "e5m2": (ml_dtypes.float8_e5m2, 14)}[fmt]
    v = np.moveaxis(np.asarray(x, np.float32).astype(ml_dtypes.bfloat16).astype(np.float64), axis, -1)
    blocks = v.reshape(v.shape[:-1] + (-1, 32))
    amax = np.abs(blocks).max(-1, keepdims=True)
    byte = np.maximum(np.where(amax > 0, np.frexp(amax)[1] - 1 + 127, 0) - down, 1)
    scale = np.exp2(byte - 127.0)
    codes = (blocks / scale).astype(np.float32).astype(dtype).astype(np.float64)
    return np.moveaxis((codes * scale).reshape(v.shape), -1, axis)


WIDE = False


def mx_kscale(k):
    if not WIDE:
        return np.ones(k)
    levels = np.array([10, -10, 5, -5, 0])
    a = np.random.permutation(np.resize(levels, k // 512 * 4)).reshape(k // 512, 4)
    idx = np.arange(k)
    return np.exp2(a[idx // 512, idx % 128 // 32])


BF16 = ml_dtypes.bfloat16


def bf(x):
    return np.asarray(x, np.float32).astype(BF16)


def f64(x):
    return np.asarray(x).astype(np.float64)


B, TW, C, MS, RED = 8, 1024, 128, 4, 1
T = TW * MS
D = C * MS
F = D * RED


def sigmoid(v):
    return 1.0 / (1.0 + np.exp(-v))


def setup_inputs():
    t = mx_kscale(F)
    return {"x": bf(np.random.standard_normal((B, T, C))),
            "w1": bf(np.random.standard_normal((D, F)) / np.sqrt(D) * t),
            "w2": bf(np.random.standard_normal((F, D)) * 3.0 / np.sqrt(F) / t[:, None])}


def reference(x, w1, w2):
    xt = f64(x).reshape(B, TW, MS, C).swapaxes(-1, -2)
    flat = xt.reshape(B, TW, D)
    h = np.maximum(mxq(flat, 2, "e4m3") @ mxq(f64(w1), 0, "e4m3"), 0.0)
    a = mxq(h, 2, "e4m3") @ mxq(f64(w2), 0, "e4m3")
    g = sigmoid(a).reshape(B, TW, C, MS)
    e = np.exp(g - g.max(-1, keepdims=True))
    y = e / e.sum(-1, keepdims=True)
    return (xt * y).sum(-1)

@@ -1,0 +1,271 @@
+from contextlib import ExitStack
+
+import concourse.bass as bass
+import concourse.mybir as mybir
+import concourse.tile as tile
+from concourse.masks import make_identity
+
+FLOPS = 2 * 2 * 8192 * 512 * 512
+
+BF16 = mybir.dt.bfloat16
+F32 = mybir.dt.float32
+U32 = mybir.dt.uint32
+U8 = mybir.dt.uint8
+FP8X4 = mybir.dt.float8_e4m3fn_x4
+ACT = mybir.ActivationFunctionType
+ALU = mybir.AluOpType
+
+P = 128
+NH = 32
+TOK = 256
+FR = 1024
+PHASES = ((0, 9), (9, 18), (18, 27), (27, 32))
+
+
+def tile_dwamformer_pa_t_kernel(tc, x, w1, w2, out):
+    nc = tc.nc
+    xf = x.flatten_outer_dims()
+    of = out.flatten_outer_dims()
+
+    with ExitStack() as ctx:
+        const = ctx.enter_context(tc.tile_pool(name="const", bufs=1))
+        xtp = ctx.enter_context(tc.tile_pool(name="xtp", bufs=7))
+        qp = ctx.enter_context(tc.tile_pool(name="qp", bufs=3))
+        hbp = ctx.enter_context(tc.tile_pool(name="hbp", bufs=2))
+        ep = ctx.enter_context(tc.tile_pool(name="ep", bufs=5))
+        prp = ctx.enter_context(tc.tile_pool(name="prp", bufs=3))
+        psx = ctx.enter_context(tc.psum_pool(name="psx", bufs=1))
+        psh = ctx.enter_context(tc.psum_pool(name="psh", bufs=2))
+        psa = ctx.enter_context(tc.psum_pool(name="psa", bufs=4))
+        psr = ctx.enter_context(tc.psum_pool(name="psr", bufs=1))
+        ctx.enter_context(tc.manual_schedule())
+
+        identb = const.tile([P, P], BF16)
+        make_identity(nc, identb[:])
+        identf = const.tile([P, P], F32)
+        make_identity(nc, identf[:])
+
+        xs_tiles = []
+        for h in range(NH):
+            x_sb = const.tile([P, 8, P], BF16, name="x_sb%d" % h)
+            xs_tiles.append(x_sb)
+
+        def load_x(h):
+            nc.sync.dma_start(
+                out=xs_tiles[h][:],
+                in_=xf[h * FR : (h + 1) * FR, :].rearrange("(j p) c -> p j c", p=P),
+            )
+
+        w1r = const.tile([P, 4, 512], BF16)
+        w2r = const.tile([P, 4, 512], BF16)
+        load_x(0)
+        nc.sync.dma_start(out=w1r[:], in_=w1.rearrange("(p j) f -> p j f", j=4))
+        load_x(1)
+        nc.sync.dma_start(out=w2r[:], in_=w2.rearrange("(p j) f -> p j f", j=4))
+        for h in range(2, NH):
+            load_x(h)
+
+        w1g = const.tile([P, 4, P, 4], BF16, align_bytes=64)
+        w2g = const.tile([P, 4, P, 4], BF16, align_bytes=64)
+        w1q = const.tile([P, 512], U32, align_bytes=64)
+        w1s = const.tile([P, 512], U8, align_bytes=64)
+        w2q = const.tile([P, 512], U32, align_bytes=64)
+        w2s = const.tile([P, 512], U8, align_bytes=64)
+        nc.scalar.copy(out=w1g[:], in_=w1r[:].rearrange("p j (q t) -> p t q j", t=4))
+        nc.scalar.copy(out=w2g[:], in_=w2r[:].rearrange("p j (q t) -> p t q j", t=4))
+
+        def quant_w(wq, ws, wg):
+            nc.vector.quantize_mx(
+                out=wq[:].bitcast(FP8X4),
+                scales=ws[:],
+                in_=wg[:].rearrange("p t q j -> p (t q j)"),
+            )
+
+        sn_tiles = []
+        for i, (h0, h1) in enumerate(PHASES):
+            sn = const.tile([P, 2, 2 * (h1 - h0), P], F32, name="sn%d" % i)
+            sn_tiles.append(sn)
+
+        def phase_of(h):
+            for i, (h0, h1) in enumerate(PHASES):
+                if h0 <= h < h1:
+                    return i, h - h0
+            raise ValueError("no phase")
+
+        st = {}
+
+        def xpose(h):
+            xb = psx.tile([P, FR], BF16)
+            for j in range(8):
+                nc.tensor.transpose(xb[:, j * P : (j + 1) * P], xs_tiles[h][:, j, :], identb[:])
+            st["xb", h] = xb
+
+        def evacx(h):
+            xt = xtp.tile([P, FR], BF16, align_bytes=64)
+            nc.vector.tensor_copy(out=xt[:], in_=st["xb", h][:])
+            st["xt", h] = xt
+
+        def quantx(h):
+            xq = qp.tile([P, TOK], U32, align_bytes=64)
+            xsc = qp.tile([P, TOK], U8, align_bytes=64)
+            nc.vector.quantize_mx(out=xq[:].bitcast(FP8X4), scales=xsc[:], in_=st["xt", h][:])
+            st["xq", h] = (xq, xsc)
+
+        def mm1(h):
+            xq, xsc = st["xq", h]
+            for s in range(2):
+                hp = psh.tile([P, 4, P], F32)
+                for t in range(4):
+                    nc.tensor.matmul_mx(
+                        out=hp[:, t, :],
+                        lhsT=w1q[:, t * P : (t + 1) * P].bitcast(FP8X4),
+                        lhsT_scale=w1s[:, t * P : (t + 1) * P],
+                        rhs=xq[:, s * P : (s + 1) * P].bitcast(FP8X4),
+                        rhs_scale=xsc[:, s * P : (s + 1) * P],
+                        start=True,
+                        stop=True,
+                    )
+                st["hp", h, s] = hp
+
+        def relu(h):
+            hb = hbp.tile([P, TOK, 4], BF16, align_bytes=64)
+            for s in range(2):
+                nc.vector.tensor_scalar_max(
+                    out=hb[:, s * P : (s + 1) * P, :],
+                    in0=st["hp", h, s][:].rearrange("p t r -> p r t"),
+                    scalar1=0.0,
+                )
+            st["hb", h] = hb
+
+        def quanth(h):
+            hq = qp.tile([P, TOK], U32, align_bytes=64)
+            hsc = qp.tile([P, TOK], U8, align_bytes=64)
+            nc.vector.quantize_mx(
+                out=hq[:].bitcast(FP8X4),
+                scales=hsc[:],
+                in_=st["hb", h][:].rearrange("p r t -> p (r t)"),
+            )
+            st["hq", h] = (hq, hsc)
+
+        def mm2(h):
+            hq, hsc = st["hq", h]
+            for u in range(2):
+                ap_ = psa.tile([P, 2, TOK], F32, name="a_ps")
+                for v in range(2):
+                    m = 2 * u + v
+                    nc.tensor.matmul_mx(
+                        out=ap_[:, v, :],
+                        lhsT=w2q[:, m * P : (m + 1) * P].bitcast(FP8X4),
+                        lhsT_scale=w2s[:, m * P : (m + 1) * P],
+                        rhs=hq[:].bitcast(FP8X4),
+                        rhs_scale=hsc[:],
+                        start=True,
+                        stop=True,
+                    )
+                st["a", h, u] = ap_
+
+        def tanh_exp(h):
+            e = ep.tile([P, 4, TOK], F32)
+            for u in range(2):
+                nc.scalar.activation(
+                    out=e[:, 2 * u : 2 * u + 2, :], in_=st["a", h, u][:], func=ACT.Tanh, scale=0.5
+                )
+            nc.scalar.activation(out=e[:], in_=e[:], func=ACT.Exp, scale=0.5)
+            st["e", h] = e
+
+        def mult(h):
+            pr = prp.tile([P, 4, TOK], F32)
+            nc.gpsimd.tensor_tensor(
+                out=pr[:],
+                in0=st["e", h][:],
+                in1=st["xt", h][:].rearrange("p (r m) -> p m r", m=4),
+                op=ALU.mult,
+            )
+            st["pr", h] = pr
+
+        def reduce_(h):
+            rp = psr.tile([P, 2, 2, P], F32)
+            for s in range(2):
+                for q, src in enumerate((st["e", h], st["pr", h])):
+                    for m in range(4):
+                        nc.tensor.matmul(
+                            out=rp[:, q, s, :],
+                            lhsT=src[:, m, s * P : (s + 1) * P],
+                            rhs=identf[:],
+                            is_transpose=True,
+                            start=(m == 0),
+                            stop=(m == 3),
+                        )
+            st["rp", h] = rp
+
+        def evacr(h):
+            i, k = phase_of(h)
+            nc.vector.tensor_copy(out=sn_tiles[i][:, :, 2 * k : 2 * k + 2, :], in_=st["rp", h][:])
+
+        def ln_(i, k0, k1):
+            s_ = sn_tiles[i][:, 0, 2 * k0 : 2 * k1, :]
+            nc.scalar.activation(out=s_, in_=s_, func=ACT.Ln)
+
+        def rexp(i, k0, k1):
+            s_ = sn_tiles[i][:, 0, 2 * k0 : 2 * k1, :]
+            nc.scalar.activation(out=s_, in_=s_, func=ACT.Exp, scale=-1.0)
+
+        def finish(i, k0, k1):
+            s_ = sn_tiles[i][:, 0, 2 * k0 : 2 * k1, :]
+            n_ = sn_tiles[i][:, 1, 2 * k0 : 2 * k1, :]
+            nc.vector.tensor_mul(out=n_, in0=n_, in1=s_)
+            r0 = (PHASES[i][0] + k0) * TOK
+            r1 = (PHASES[i][0] + k1) * TOK
+            nc.sync.dma_start(out=of[r0:r1, :].rearrange("(n p) c -> p n c", p=P), in_=n_)
+
+        NPER = NH + 8
+        act_late = [[] for t in range(NPER + 8)]
+        dve_early = [[] for t in range(NPER + 8)]
+        for i, (h0, h1) in enumerate(PHASES[:-1]):
+            t0 = h1 - 1 + 5
+            act_late[t0].append((ln_, i, 0, h1 - h0))
+            for c, k0 in enumerate(range(0, h1 - h0, 3)):
+                k1 = min(k0 + 3, h1 - h0)
+                act_late[t0 + 1 + c].append((rexp, i, k0, k1))
+                dve_early[t0 + 3 + c].append((finish, i, k0, k1))
+        il = len(PHASES) - 1
+        l0, l1 = PHASES[il]
+        tl = NH + 1
+        kdone = tl - 5 - l0 + 1
+        act_late[tl].append((ln_, il, 0, kdone))
+        act_late[tl].append((rexp, il, 0, kdone))
+        dve_early[tl + 1].append((finish, il, 0, kdone))
+        for k in range(kdone, l1 - l0):
+            tk = l0 + k + 5
+            act_late[tk].append((ln_, il, k, k + 1))
+            act_late[tk].append((rexp, il, k, k + 1))
+            dve_early[tk + 1].append((finish, il, k, k + 1))
+
+        for t in range(NPER):
+            if 0 <= t - 5 < NH:
+                evacr(t - 5)
+            for f, i, k0, k1 in dve_early[t]:
+                f(i, k0, k1)
+            if t < NH:
+                xpose(t)
+                evacx(t)
+            if 0 <= t - 1 < NH:
+                mm1(t - 1)
+                relu(t - 1)
+            if t < NH:
+                quantx(t)
+            if t == 0:
+                quant_w(w1q, w1s, w1g)
+            if t == 1:
+                quant_w(w2q, w2s, w2g)
+            if 0 <= t - 2 < NH:
+                mm2(t - 2)
+            if 0 <= t - 1 < NH:
+                quanth(t - 1)
+            if 0 <= t - 2 < NH:
+                tanh_exp(t - 2)
+                mult(t - 2)
+            for f, i, k0, k1 in act_late[t]:
+                f(i, k0, k1)
+            if 0 <= t - 4 < NH:
+                reduce_(t - 4)

@@ -36,8 +36,8 @@ def tile_dwamformer_pa_t_kernel(tc, x, w1, w2, out):
         prp = ctx.enter_context(tc.tile_pool(name="prp", bufs=3))
         psx = ctx.enter_context(tc.psum_pool(name="psx", bufs=1))
         psh = ctx.enter_context(tc.psum_pool(name="psh", bufs=2))
-        psa = ctx.enter_context(tc.psum_pool(name="psa", bufs=4))
-        psr = ctx.enter_context(tc.psum_pool(name="psr", bufs=1))
+        psa = ctx.enter_context(tc.psum_pool(name="psa", bufs=3))
+        psr = ctx.enter_context(tc.psum_pool(name="psr", bufs=2))
         ctx.enter_context(tc.manual_schedule())
 
         identb = const.tile([P, P], BF16)
@@ -183,20 +183,22 @@ def tile_dwamformer_pa_t_kernel(tc, x, w1, w2, out):
             )
             st["pr", h] = pr
 
-        def reduce_(h):
-            rp = psr.tile([P, 2, 2, P], F32)
-            for s in range(2):
-                for q, src in enumerate((st["e", h], st["pr", h])):
-                    for m in range(4):
-                        nc.tensor.matmul(
-                            out=rp[:, q, s, :],
-                            lhsT=src[:, m, s * P : (s + 1) * P],
-                            rhs=identf[:],
-                            is_transpose=True,
-                            start=(m == 0),
-                            stop=(m == 3),
-                        )
-            st["rp", h] = rp
+        def reduce_(h, groups):
+            if ("rp", h) not in st:
+                rp = psr.tile([P, 2, 2, P], F32)
+                st["rp", h] = rp
+            rp = st["rp", h]
+            for q, s in groups:
+                src = st["e", h] if q == 0 else st["pr", h]
+                for m in range(4):
+                    nc.tensor.matmul(
+                        out=rp[:, q, s, :],
+                        lhsT=src[:, m, s * P : (s + 1) * P],
+                        rhs=identf[:],
+                        is_transpose=True,
+                        start=(m == 0),
+                        stop=(m == 3),
+                    )
 
         def evacr(h):
             i, k = phase_of(h)
@@ -222,7 +224,7 @@ def tile_dwamformer_pa_t_kernel(tc, x, w1, w2, out):
         act_late = [[] for t in range(NPER + 8)]
         dve_early = [[] for t in range(NPER + 8)]
         for i, (h0, h1) in enumerate(PHASES[:-1]):
-            t0 = h1 - 1 + 5
+            t0 = h1 - 1 + 4
             act_late[t0].append((ln_, i, 0, h1 - h0))
             for c, k0 in enumerate(range(0, h1 - h0, 3)):
                 k1 = min(k0 + 3, h1 - h0)
@@ -231,27 +233,34 @@ def tile_dwamformer_pa_t_kernel(tc, x, w1, w2, out):
         il = len(PHASES) - 1
         l0, l1 = PHASES[il]
         tl = NH + 1
-        kdone = tl - 5 - l0 + 1
+        kdone = tl - 4 - l0 + 1
         act_late[tl].append((ln_, il, 0, kdone))
         act_late[tl].append((rexp, il, 0, kdone))
         dve_early[tl + 1].append((finish, il, 0, kdone))
         for k in range(kdone, l1 - l0):
-            tk = l0 + k + 5
+            tk = l0 + k + 4
             act_late[tk].append((ln_, il, k, k + 1))
             act_late[tk].append((rexp, il, k, k + 1))
             dve_early[tk + 1].append((finish, il, k, k + 1))
 
         for t in range(NPER):
-            if 0 <= t - 5 < NH:
-                evacr(t - 5)
-            for f, i, k0, k1 in dve_early[t]:
-                f(i, k0, k1)
+            if t < NH + 2:
+                for f, i, k0, k1 in dve_early[t]:
+                    f(i, k0, k1)
             if t < NH:
                 xpose(t)
                 evacx(t)
+            if 0 <= t - 4 < NH:
+                reduce_(t - 4, ((0, 0),))
             if 0 <= t - 1 < NH:
                 mm1(t - 1)
                 relu(t - 1)
+            if 0 <= t - 4 < NH:
+                reduce_(t - 4, ((0, 1), (1, 0), (1, 1)))
+                evacr(t - 4)
+            if t >= NH + 2:
+                for f, i, k0, k1 in dve_early[t]:
+                    f(i, k0, k1)
             if t < NH:
                 quantx(t)
             if t == 0:
@@ -267,5 +276,3 @@ def tile_dwamformer_pa_t_kernel(tc, x, w1, w2, out):
                 mult(t - 2)
             for f, i, k0, k1 in act_late[t]:
                 f(i, k0, k1)
-            if 0 <= t - 4 < NH:
-                reduce_(t - 4)

@@ -19,7 +19,7 @@ P = 128
 NH = 32
 TOK = 256
 FR = 1024
-PHASES = ((0, 9), (9, 18), (18, 27), (27, 32))
+PHASES = ((0, 21), (21, 32))
 
 
 def tile_dwamformer_pa_t_kernel(tc, x, w1, w2, out):
@@ -33,7 +33,7 @@ def tile_dwamformer_pa_t_kernel(tc, x, w1, w2, out):
         qp = ctx.enter_context(tc.tile_pool(name="qp", bufs=3))
         hbp = ctx.enter_context(tc.tile_pool(name="hbp", bufs=2))
         ep = ctx.enter_context(tc.tile_pool(name="ep", bufs=5))
-        prp = ctx.enter_context(tc.tile_pool(name="prp", bufs=3))
+        prp = ctx.enter_context(tc.tile_pool(name="prp", bufs=2))
         psx = ctx.enter_context(tc.psum_pool(name="psx", bufs=1))
         psh = ctx.enter_context(tc.psum_pool(name="psh", bufs=2))
         psa = ctx.enter_context(tc.psum_pool(name="psa", bufs=3))
@@ -71,8 +71,7 @@ def tile_dwamformer_pa_t_kernel(tc, x, w1, w2, out):
         w1s = const.tile([P, 512], U8, align_bytes=64)
         w2q = const.tile([P, 512], U32, align_bytes=64)
         w2s = const.tile([P, 512], U8, align_bytes=64)
-        nc.scalar.copy(out=w1g[:], in_=w1r[:].rearrange("p j (q t) -> p t q j", t=4))
-        nc.scalar.copy(out=w2g[:], in_=w2r[:].rearrange("p j (q t) -> p t q j", t=4))
+        nc.vector.tensor_copy(out=w1g[:], in_=w1r[:].rearrange("p j (q t) -> p t q j", t=4))
 
         def quant_w(wq, ws, wg):
             nc.vector.quantize_mx(
@@ -102,7 +101,7 @@ def tile_dwamformer_pa_t_kernel(tc, x, w1, w2, out):
 
         def evacx(h):
             xt = xtp.tile([P, FR], BF16, align_bytes=64)
-            nc.vector.tensor_copy(out=xt[:], in_=st["xb", h][:])
+            nc.scalar.copy(out=xt[:], in_=st["xb", h][:])
             st["xt", h] = xt
 
         def quantx(h):
@@ -164,18 +163,21 @@ def tile_dwamformer_pa_t_kernel(tc, x, w1, w2, out):
                     )
                 st["a", h, u] = ap_
 
-        def tanh_exp(h):
+        def tanh_(h):
             e = ep.tile([P, 4, TOK], F32)
             for u in range(2):
                 nc.scalar.activation(
                     out=e[:, 2 * u : 2 * u + 2, :], in_=st["a", h, u][:], func=ACT.Tanh, scale=0.5
                 )
-            nc.scalar.activation(out=e[:], in_=e[:], func=ACT.Exp, scale=0.5)
             st["e", h] = e
+
+        def exp_(h):
+            e = st["e", h]
+            nc.scalar.activation(out=e[:], in_=e[:], func=ACT.Exp, scale=0.5)
 
         def mult(h):
             pr = prp.tile([P, 4, TOK], F32)
-            nc.gpsimd.tensor_tensor(
+            nc.vector.tensor_tensor(
                 out=pr[:],
                 in0=st["e", h][:],
                 in1=st["xt", h][:].rearrange("p (r m) -> p m r", m=4),
@@ -222,49 +224,58 @@ def tile_dwamformer_pa_t_kernel(tc, x, w1, w2, out):
 
         NPER = NH + 8
         act_late = [[] for t in range(NPER + 8)]
-        dve_early = [[] for t in range(NPER + 8)]
+        dve_mid = [[] for t in range(NPER + 8)]
         for i, (h0, h1) in enumerate(PHASES[:-1]):
-            t0 = h1 - 1 + 4
+            t0 = h1 - 1 + 5
             act_late[t0].append((ln_, i, 0, h1 - h0))
             for c, k0 in enumerate(range(0, h1 - h0, 3)):
                 k1 = min(k0 + 3, h1 - h0)
                 act_late[t0 + 1 + c].append((rexp, i, k0, k1))
-                dve_early[t0 + 3 + c].append((finish, i, k0, k1))
+                dve_mid[t0 + 2 + c].append((finish, i, k0, k1))
         il = len(PHASES) - 1
         l0, l1 = PHASES[il]
-        tl = NH + 1
-        kdone = tl - 4 - l0 + 1
-        act_late[tl].append((ln_, il, 0, kdone))
-        act_late[tl].append((rexp, il, 0, kdone))
-        dve_early[tl + 1].append((finish, il, 0, kdone))
+        tl = NH + 2
+        kdone = tl - 5 - l0 + 1
+        for k0 in range(0, kdone, 2):
+            k1 = min(k0 + 2, kdone)
+            act_late[tl].append((ln_, il, k0, k1))
+            act_late[tl].append((rexp, il, k0, k1))
+            dve_mid[tl + 1].append((finish, il, k0, k1))
         for k in range(kdone, l1 - l0):
-            tk = l0 + k + 4
+            tk = l0 + k + 5
             act_late[tk].append((ln_, il, k, k + 1))
             act_late[tk].append((rexp, il, k, k + 1))
-            dve_early[tk + 1].append((finish, il, k, k + 1))
+            dve_mid[tk + 1].append((finish, il, k, k + 1))
 
         for t in range(NPER):
-            if t < NH + 2:
-                for f, i, k0, k1 in dve_early[t]:
-                    f(i, k0, k1)
+            if 0 <= t - 4 < NH:
+                mult(t - 4)
             if t < NH:
                 xpose(t)
                 evacx(t)
+            if t == 0:
+                nc.scalar.copy(out=w2g[:], in_=w2r[:].rearrange("p j (q t) -> p t q j", t=4))
+                quant_w(w1q, w1s, w1g)
             if 0 <= t - 4 < NH:
                 reduce_(t - 4, ((0, 0),))
+            if t < NH:
+                quantx(t)
+            if t < NH + 2:
+                for f, i, k0, k1 in dve_mid[t]:
+                    f(i, k0, k1)
             if 0 <= t - 1 < NH:
                 mm1(t - 1)
                 relu(t - 1)
+            if 0 <= t - 3 < NH:
+                exp_(t - 3)
+            for f, i, k0, k1 in act_late[t]:
+                f(i, k0, k1)
             if 0 <= t - 4 < NH:
                 reduce_(t - 4, ((0, 1), (1, 0), (1, 1)))
                 evacr(t - 4)
             if t >= NH + 2:
-                for f, i, k0, k1 in dve_early[t]:
+                for f, i, k0, k1 in dve_mid[t]:
                     f(i, k0, k1)
-            if t < NH:
-                quantx(t)
-            if t == 0:
-                quant_w(w1q, w1s, w1g)
             if t == 1:
                 quant_w(w2q, w2s, w2g)
             if 0 <= t - 2 < NH:
@@ -272,7 +283,4 @@ def tile_dwamformer_pa_t_kernel(tc, x, w1, w2, out):
             if 0 <= t - 1 < NH:
                 quanth(t - 1)
             if 0 <= t - 2 < NH:
-                tanh_exp(t - 2)
-                mult(t - 2)
-            for f, i, k0, k1 in act_late[t]:
-                f(i, k0, k1)
+                tanh_(t - 2)

@@ -51,10 +51,9 @@ def tile_dwamformer_pa_t_kernel(tc, x, w1, w2, out):
             xs_tiles.append(x_sb)
 
         def load_x(h):
-            nc.sync.dma_start(
-                out=xs_tiles[h][:],
-                in_=xf[h * FR : (h + 1) * FR, :].rearrange("(j p) c -> p j c", p=P),
-            )
+            for j in range(8):
+                r0 = h * FR + j * P
+                nc.sync.dma_start(out=xs_tiles[h][:, j, :], in_=xf[r0 : r0 + P, :])
 
         w1r = const.tile([P, 4, 512], BF16)
         w2r = const.tile([P, 4, 512], BF16)
@@ -258,14 +257,14 @@ def tile_dwamformer_pa_t_kernel(tc, x, w1, w2, out):
                 quant_w(w1q, w1s, w1g)
             if 0 <= t - 4 < NH:
                 reduce_(t - 4, ((0, 0),))
-            if t < NH:
-                quantx(t)
             if t < NH + 2:
                 for f, i, k0, k1 in dve_mid[t]:
                     f(i, k0, k1)
             if 0 <= t - 1 < NH:
                 mm1(t - 1)
                 relu(t - 1)
+            if t < NH:
+                quantx(t)
             if 0 <= t - 3 < NH:
                 exp_(t - 3)
             for f, i, k0, k1 in act_late[t]:

@@ -36,8 +36,9 @@ def tile_dwamformer_pa_t_kernel(tc, x, w1, w2, out):
         prp = ctx.enter_context(tc.tile_pool(name="prp", bufs=2))
         psx = ctx.enter_context(tc.psum_pool(name="psx", bufs=1))
         psh = ctx.enter_context(tc.psum_pool(name="psh", bufs=2))
-        psa = ctx.enter_context(tc.psum_pool(name="psa", bufs=3))
+        psa = ctx.enter_context(tc.psum_pool(name="psa", bufs=2))
         psr = ctx.enter_context(tc.psum_pool(name="psr", bufs=2))
+        psd = ctx.enter_context(tc.psum_pool(name="psd", bufs=1))
         ctx.enter_context(tc.manual_schedule())
 
         identb = const.tile([P, P], BF16)
@@ -162,6 +163,19 @@ def tile_dwamformer_pa_t_kernel(tc, x, w1, w2, out):
                     )
                 st["a", h, u] = ap_
 
+        scr = psd.tile([P, 512], F32)
+
+        def keep_clock():
+            nc.tensor.matmul_mx(
+                out=scr[:],
+                lhsT=w1q[:, 0:P].bitcast(FP8X4),
+                lhsT_scale=w1s[:, 0:P],
+                rhs=w1q[:].bitcast(FP8X4),
+                rhs_scale=w1s[:],
+                start=True,
+                stop=True,
+            )
+
         def tanh_(h):
             e = ep.tile([P, 4, TOK], F32)
             for u in range(2):
@@ -263,6 +277,8 @@ def tile_dwamformer_pa_t_kernel(tc, x, w1, w2, out):
             if 0 <= t - 1 < NH:
                 mm1(t - 1)
                 relu(t - 1)
+            if 1 <= t < NH + 5:
+                keep_clock()
             if t < NH:
                 quantx(t)
             if 0 <= t - 3 < NH:
@@ -279,6 +295,8 @@ def tile_dwamformer_pa_t_kernel(tc, x, w1, w2, out):
                 quant_w(w2q, w2s, w2g)
             if 0 <= t - 2 < NH:
                 mm2(t - 2)
+            if 1 <= t < NH + 4:
+                keep_clock()
             if 0 <= t - 1 < NH:
                 quanth(t - 1)
             if 0 <= t - 2 < NH:

@@ -19,7 +19,10 @@ P = 128
 NH = 32
 TOK = 256
 FR = 1024
-PHASES = ((0, 21), (21, 32))
+MID_CHUNKS = ((0, 3), (3, 6), (6, 9), (9, 12), (12, 15), (15, 18), (18, 21))
+END_CHUNKS = ((21, 24), (24, 27), (27, 30))
+N_ACT = 30
+PHASES = MID_CHUNKS + END_CHUNKS
 
 
 def tile_dwamformer_pa_t_kernel(tc, x, w1, w2, out):
@@ -36,9 +39,8 @@ def tile_dwamformer_pa_t_kernel(tc, x, w1, w2, out):
         prp = ctx.enter_context(tc.tile_pool(name="prp", bufs=2))
         psx = ctx.enter_context(tc.psum_pool(name="psx", bufs=1))
         psh = ctx.enter_context(tc.psum_pool(name="psh", bufs=2))
-        psa = ctx.enter_context(tc.psum_pool(name="psa", bufs=2))
+        psa = ctx.enter_context(tc.psum_pool(name="psa", bufs=3))
         psr = ctx.enter_context(tc.psum_pool(name="psr", bufs=2))
-        psd = ctx.enter_context(tc.psum_pool(name="psd", bufs=1))
         ctx.enter_context(tc.manual_schedule())
 
         identb = const.tile([P, P], BF16)
@@ -101,7 +103,7 @@ def tile_dwamformer_pa_t_kernel(tc, x, w1, w2, out):
 
         def evacx(h):
             xt = xtp.tile([P, FR], BF16, align_bytes=64)
-            nc.scalar.copy(out=xt[:], in_=st["xb", h][:])
+            nc.vector.tensor_copy(out=xt[:], in_=st["xb", h][:])
             st["xt", h] = xt
 
         def quantx(h):
@@ -163,19 +165,6 @@ def tile_dwamformer_pa_t_kernel(tc, x, w1, w2, out):
                     )
                 st["a", h, u] = ap_
 
-        scr = psd.tile([P, 512], F32)
-
-        def keep_clock():
-            nc.tensor.matmul_mx(
-                out=scr[:],
-                lhsT=w1q[:, 0:P].bitcast(FP8X4),
-                lhsT_scale=w1s[:, 0:P],
-                rhs=w1q[:].bitcast(FP8X4),
-                rhs_scale=w1s[:],
-                start=True,
-                stop=True,
-            )
-
         def tanh_(h):
             e = ep.tile([P, 4, TOK], F32)
             for u in range(2):
@@ -217,7 +206,17 @@ def tile_dwamformer_pa_t_kernel(tc, x, w1, w2, out):
 
         def evacr(h):
             i, k = phase_of(h)
-            nc.vector.tensor_copy(out=sn_tiles[i][:, :, 2 * k : 2 * k + 2, :], in_=st["rp", h][:])
+            nc.scalar.copy(out=sn_tiles[i][:, :, 2 * k : 2 * k + 2, :], in_=st["rp", h][:])
+
+        def direct(h):
+            rp = st["rp", h]
+            rc = prp.tile([P, 2, P], F32)
+            nc.vector.reciprocal(out=rc[:], in_=rp[:, 0, :, :])
+            ot = prp.tile([P, 2, P], F32)
+            nc.vector.tensor_mul(out=ot[:], in0=rp[:, 1, :, :], in1=rc[:])
+            nc.sync.dma_start(
+                out=of[h * TOK : (h + 1) * TOK, :].rearrange("(n p) c -> p n c", p=P), in_=ot[:]
+            )
 
         def ln_(i, k0, k1):
             s_ = sn_tiles[i][:, 0, 2 * k0 : 2 * k1, :]
@@ -236,33 +235,21 @@ def tile_dwamformer_pa_t_kernel(tc, x, w1, w2, out):
             nc.sync.dma_start(out=of[r0:r1, :].rearrange("(n p) c -> p n c", p=P), in_=n_)
 
         NPER = NH + 8
-        act_late = [[] for t in range(NPER + 8)]
-        dve_mid = [[] for t in range(NPER + 8)]
-        for i, (h0, h1) in enumerate(PHASES[:-1]):
-            t0 = h1 - 1 + 5
-            act_late[t0].append((ln_, i, 0, h1 - h0))
-            for c, k0 in enumerate(range(0, h1 - h0, 3)):
-                k1 = min(k0 + 3, h1 - h0)
-                act_late[t0 + 1 + c].append((rexp, i, k0, k1))
-                dve_mid[t0 + 2 + c].append((finish, i, k0, k1))
-        il = len(PHASES) - 1
-        l0, l1 = PHASES[il]
+        act_slot = [[] for t in range(NPER + 8)]
+        dve_slot = [[] for t in range(NPER + 8)]
+        t0 = MID_CHUNKS[-1][1] - 1 + 5
+        for i, (h0, h1) in enumerate(MID_CHUNKS):
+            act_slot[t0].append((ln_, i, 0, h1 - h0))
+            act_slot[t0 + 1 + i].append((rexp, i, 0, h1 - h0))
+            dve_slot[t0 + 2 + i].append((finish, i, 0, h1 - h0))
         tl = NH + 2
-        kdone = tl - 5 - l0 + 1
-        for k0 in range(0, kdone, 2):
-            k1 = min(k0 + 2, kdone)
-            act_late[tl].append((ln_, il, k0, k1))
-            act_late[tl].append((rexp, il, k0, k1))
-            dve_mid[tl + 1].append((finish, il, k0, k1))
-        for k in range(kdone, l1 - l0):
-            tk = l0 + k + 5
-            act_late[tk].append((ln_, il, k, k + 1))
-            act_late[tk].append((rexp, il, k, k + 1))
-            dve_mid[tk + 1].append((finish, il, k, k + 1))
+        for j, (h0, h1) in enumerate(END_CHUNKS):
+            act_slot[tl].append((ln_, len(MID_CHUNKS) + j, 0, h1 - h0))
+        for j, (h0, h1) in enumerate(END_CHUNKS):
+            act_slot[tl].append((rexp, len(MID_CHUNKS) + j, 0, h1 - h0))
+            dve_slot[tl + 2].append((finish, len(MID_CHUNKS) + j, 0, h1 - h0))
 
         for t in range(NPER):
-            if 0 <= t - 4 < NH:
-                mult(t - 4)
             if t < NH:
                 xpose(t)
                 evacx(t)
@@ -271,32 +258,28 @@ def tile_dwamformer_pa_t_kernel(tc, x, w1, w2, out):
                 quant_w(w1q, w1s, w1g)
             if 0 <= t - 4 < NH:
                 reduce_(t - 4, ((0, 0),))
-            if t < NH + 2:
-                for f, i, k0, k1 in dve_mid[t]:
-                    f(i, k0, k1)
+            for f, i, k0, k1 in dve_slot[t]:
+                f(i, k0, k1)
             if 0 <= t - 1 < NH:
                 mm1(t - 1)
                 relu(t - 1)
-            if 1 <= t < NH + 5:
-                keep_clock()
             if t < NH:
                 quantx(t)
             if 0 <= t - 3 < NH:
                 exp_(t - 3)
-            for f, i, k0, k1 in act_late[t]:
+                mult(t - 3)
+            for f, i, k0, k1 in act_slot[t]:
                 f(i, k0, k1)
             if 0 <= t - 4 < NH:
                 reduce_(t - 4, ((0, 1), (1, 0), (1, 1)))
-                evacr(t - 4)
-            if t >= NH + 2:
-                for f, i, k0, k1 in dve_mid[t]:
-                    f(i, k0, k1)
+                if t - 4 < N_ACT:
+                    evacr(t - 4)
+                else:
+                    direct(t - 4)
             if t == 1:
                 quant_w(w2q, w2s, w2g)
             if 0 <= t - 2 < NH:
                 mm2(t - 2)
-            if 1 <= t < NH + 4:
-                keep_clock()
             if 0 <= t - 1 < NH:
                 quanth(t - 1)
             if 0 <= t - 2 < NH:

@@ -34,9 +34,10 @@ def tile_dwamformer_pa_t_kernel(tc, x, w1, w2, out):
         const = ctx.enter_context(tc.tile_pool(name="const", bufs=1))
         xtp = ctx.enter_context(tc.tile_pool(name="xtp", bufs=7))
         qp = ctx.enter_context(tc.tile_pool(name="qp", bufs=3))
-        hbp = ctx.enter_context(tc.tile_pool(name="hbp", bufs=2))
-        ep = ctx.enter_context(tc.tile_pool(name="ep", bufs=5))
-        prp = ctx.enter_context(tc.tile_pool(name="prp", bufs=2))
+        hbp = ctx.enter_context(tc.tile_pool(name="hbp", bufs=3))
+        ep = ctx.enter_context(tc.tile_pool(name="ep", bufs=6))
+        prp = ctx.enter_context(tc.tile_pool(name="prp", bufs=3))
+        smp = ctx.enter_context(tc.tile_pool(name="smp", bufs=2))
         psx = ctx.enter_context(tc.psum_pool(name="psx", bufs=1))
         psh = ctx.enter_context(tc.psum_pool(name="psh", bufs=2))
         psa = ctx.enter_context(tc.psum_pool(name="psa", bufs=3))
@@ -60,8 +61,8 @@ def tile_dwamformer_pa_t_kernel(tc, x, w1, w2, out):
 
         w1r = const.tile([P, 4, 512], BF16)
         w2r = const.tile([P, 4, 512], BF16)
-        load_x(0)
         nc.sync.dma_start(out=w1r[:], in_=w1.rearrange("(p j) f -> p j f", j=4))
+        load_x(0)
         load_x(1)
         nc.sync.dma_start(out=w2r[:], in_=w2.rearrange("(p j) f -> p j f", j=4))
         for h in range(2, NH):
@@ -73,7 +74,10 @@ def tile_dwamformer_pa_t_kernel(tc, x, w1, w2, out):
         w1s = const.tile([P, 512], U8, align_bytes=64)
         w2q = const.tile([P, 512], U32, align_bytes=64)
         w2s = const.tile([P, 512], U8, align_bytes=64)
-        nc.vector.tensor_copy(out=w1g[:], in_=w1r[:].rearrange("p j (q t) -> p t q j", t=4))
+        w1v = w1r[:].rearrange("p j (q t) -> p t q j", t=4)
+        nc.vector.tensor_copy(out=w1g[:, 0:2, :, :], in_=w1v[:, 0:2, :, :])
+        nc.scalar.copy(out=w1g[:, 2:4, :, :], in_=w1v[:, 2:4, :, :])
+        nc.scalar.copy(out=w2g[:], in_=w2r[:].rearrange("p j (q t) -> p t q j", t=4))
 
         def quant_w(wq, ws, wg):
             nc.vector.quantize_mx(
@@ -130,13 +134,17 @@ def tile_dwamformer_pa_t_kernel(tc, x, w1, w2, out):
 
         def relu(h):
             hb = hbp.tile([P, TOK, 4], BF16, align_bytes=64)
-            for s in range(2):
-                nc.vector.tensor_scalar_max(
-                    out=hb[:, s * P : (s + 1) * P, :],
-                    in0=st["hp", h, s][:].rearrange("p t r -> p r t"),
-                    scalar1=0.0,
-                )
+            nc.vector.tensor_scalar_max(
+                out=hb[:, 0:P, :], in0=st["hp", h, 0][:].rearrange("p t r -> p r t"), scalar1=0.0
+            )
             st["hb", h] = hb
+
+        def relu_act(h):
+            nc.scalar.activation(
+                out=st["hb", h][:, P : 2 * P, :],
+                in_=st["hp", h, 1][:].rearrange("p t r -> p r t"),
+                func=ACT.Relu,
+            )
 
         def quanth(h):
             hq = qp.tile([P, TOK], U32, align_bytes=64)
@@ -187,22 +195,29 @@ def tile_dwamformer_pa_t_kernel(tc, x, w1, w2, out):
             )
             st["pr", h] = pr
 
-        def reduce_(h, groups):
-            if ("rp", h) not in st:
-                rp = psr.tile([P, 2, 2, P], F32)
-                st["rp", h] = rp
+        def pre(h):
+            e = st["e", h]
+            s2 = prp.tile([P, 2, TOK], F32)
+            nc.vector.tensor_add(out=s2[:], in0=e[:, 0:2, :], in1=e[:, 2:4, :])
+            st["s2", h] = s2
+
+        def add_up(dst, parts):
+            n = len(parts)
+            for k, part in enumerate(parts):
+                nc.tensor.matmul(
+                    out=dst, lhsT=part, rhs=identf[:], is_transpose=True, start=(k == 0), stop=(k == n - 1)
+                )
+
+        def reduce_first(h):
+            rp = psr.tile([P, 2, 2, P], F32)
+            st["rp", h] = rp
+            add_up(rp[:, 0, 0, :], [st["s2", h][:, k, 0:P] for k in range(2)])
+
+        def reduce_rest(h):
             rp = st["rp", h]
-            for q, s in groups:
-                src = st["e", h] if q == 0 else st["pr", h]
-                for m in range(4):
-                    nc.tensor.matmul(
-                        out=rp[:, q, s, :],
-                        lhsT=src[:, m, s * P : (s + 1) * P],
-                        rhs=identf[:],
-                        is_transpose=True,
-                        start=(m == 0),
-                        stop=(m == 3),
-                    )
+            add_up(rp[:, 0, 1, :], [st["s2", h][:, k, P : 2 * P] for k in range(2)])
+            for s in range(2):
+                add_up(rp[:, 1, s, :], [st["pr", h][:, m, s * P : (s + 1) * P] for m in range(4)])
 
         def evacr(h):
             i, k = phase_of(h)
@@ -210,9 +225,9 @@ def tile_dwamformer_pa_t_kernel(tc, x, w1, w2, out):
 
         def direct(h):
             rp = st["rp", h]
-            rc = prp.tile([P, 2, P], F32)
+            rc = smp.tile([P, 2, P], F32)
             nc.vector.reciprocal(out=rc[:], in_=rp[:, 0, :, :])
-            ot = prp.tile([P, 2, P], F32)
+            ot = smp.tile([P, 2, P], F32)
             nc.vector.tensor_mul(out=ot[:], in0=rp[:, 1, :, :], in1=rc[:])
             nc.sync.dma_start(
                 out=of[h * TOK : (h + 1) * TOK, :].rearrange("(n p) c -> p n c", p=P), in_=ot[:]
@@ -234,53 +249,63 @@ def tile_dwamformer_pa_t_kernel(tc, x, w1, w2, out):
             r1 = (PHASES[i][0] + k1) * TOK
             nc.sync.dma_start(out=of[r0:r1, :].rearrange("(n p) c -> p n c", p=P), in_=n_)
 
-        NPER = NH + 8
+        NPER = NH + 9
         act_slot = [[] for t in range(NPER + 8)]
         dve_slot = [[] for t in range(NPER + 8)]
-        t0 = MID_CHUNKS[-1][1] - 1 + 5
+        t0 = MID_CHUNKS[-1][1] - 1 + 6
         for i, (h0, h1) in enumerate(MID_CHUNKS):
             act_slot[t0].append((ln_, i, 0, h1 - h0))
             act_slot[t0 + 1 + i].append((rexp, i, 0, h1 - h0))
             dve_slot[t0 + 2 + i].append((finish, i, 0, h1 - h0))
-        tl = NH + 2
+        tl = N_ACT - 1 + 6
         for j, (h0, h1) in enumerate(END_CHUNKS):
             act_slot[tl].append((ln_, len(MID_CHUNKS) + j, 0, h1 - h0))
         for j, (h0, h1) in enumerate(END_CHUNKS):
             act_slot[tl].append((rexp, len(MID_CHUNKS) + j, 0, h1 - h0))
             dve_slot[tl + 2].append((finish, len(MID_CHUNKS) + j, 0, h1 - h0))
 
+        def on(h):
+            return 0 <= h < NH
+
         for t in range(NPER):
-            if t < NH:
+            if on(t):
                 xpose(t)
+            if on(t - 5):
+                reduce_first(t - 5)
+            if on(t - 1):
+                mm1(t - 1)
+            if on(t - 2):
+                quanth(t - 2)
+            if on(t - 5):
+                reduce_rest(t - 5)
+            if on(t):
                 evacx(t)
             if t == 0:
-                nc.scalar.copy(out=w2g[:], in_=w2r[:].rearrange("p j (q t) -> p t q j", t=4))
                 quant_w(w1q, w1s, w1g)
-            if 0 <= t - 4 < NH:
-                reduce_(t - 4, ((0, 0),))
-            for f, i, k0, k1 in dve_slot[t]:
-                f(i, k0, k1)
-            if 0 <= t - 1 < NH:
-                mm1(t - 1)
-                relu(t - 1)
-            if t < NH:
+            if on(t - 4):
+                pre(t - 4)
+            if on(t):
                 quantx(t)
-            if 0 <= t - 3 < NH:
-                exp_(t - 3)
-                mult(t - 3)
-            for f, i, k0, k1 in act_slot[t]:
-                f(i, k0, k1)
-            if 0 <= t - 4 < NH:
-                reduce_(t - 4, ((0, 1), (1, 0), (1, 1)))
-                if t - 4 < N_ACT:
-                    evacr(t - 4)
-                else:
-                    direct(t - 4)
+            if on(t - 1):
+                relu(t - 1)
             if t == 1:
                 quant_w(w2q, w2s, w2g)
-            if 0 <= t - 2 < NH:
+            if on(t - 2):
                 mm2(t - 2)
-            if 0 <= t - 1 < NH:
-                quanth(t - 1)
-            if 0 <= t - 2 < NH:
+            if on(t - 1):
+                relu_act(t - 1)
+            if on(t - 3):
+                exp_(t - 3)
+            if on(t - 4):
+                mult(t - 4)
+            for f, i, k0, k1 in dve_slot[t]:
+                f(i, k0, k1)
+            for f, i, k0, k1 in act_slot[t]:
+                f(i, k0, k1)
+            if on(t - 5):
+                if t - 5 < N_ACT:
+                    evacr(t - 5)
+                else:
+                    direct(t - 5)
+            if on(t - 2):
                 tanh_(t - 2)

@@ -1,8 +1,6 @@
 from contextlib import ExitStack
 
-import concourse.bass as bass
 import concourse.mybir as mybir
-import concourse.tile as tile
 from concourse.masks import make_identity
 
 FLOPS = 2 * 2 * 8192 * 512 * 512
@@ -13,299 +11,323 @@ U32 = mybir.dt.uint32
 U8 = mybir.dt.uint8
 FP8X4 = mybir.dt.float8_e4m3fn_x4
 ACT = mybir.ActivationFunctionType
-ALU = mybir.AluOpType
 
 P = 128
-NH = 32
-TOK = 256
-FR = 1024
-MID_CHUNKS = ((0, 3), (3, 6), (6, 9), (9, 12), (12, 15), (15, 18), (18, 21))
-END_CHUNKS = ((21, 24), (24, 27), (27, 30))
-N_ACT = 30
-PHASES = MID_CHUNKS + END_CHUNKS
+PACK = 4
+SLABS = 32
+WIN = 256
+FRAMES = WIN * PACK
+HALVES = WIN // P
+
+LAG_X = 0
+LAG_MM1 = 1
+LAG_MM2 = 2
+LAG_EXP = 3
+LAG_PROD = 4
+LAG_SUMS = 5
+
+FIRST_LN = ((0, 3), (3, 6), (6, 9), (9, 12), (12, 15), (15, 18), (18, 21))
+SECOND_LN = ((21, 24), (24, 27), (27, 30))
+GROUPS = FIRST_LN + SECOND_LN
+END_FIRST = 21
+BY_RECIPROCAL = 30
+STEP_LN1 = END_FIRST + LAG_SUMS
+STEP_LN2 = BY_RECIPROCAL + LAG_SUMS
+assert STEP_LN1 + len(FIRST_LN) == SLABS - 1 + LAG_MM2
+RELU_ALL_ON_VECTOR = (STEP_LN1 - 1 - LAG_MM1, STEP_LN1 + 2 - LAG_MM1)
+SUMS_OUT_ON_VECTOR = (STEP_LN1 - LAG_SUMS, STEP_LN1 + 4 - LAG_SUMS)
+STEPS = STEP_LN2 + 3
+
+
+def within(s, span):
+    return span[0] <= s < span[1]
 
 
 def tile_dwamformer_pa_t_kernel(tc, x, w1, w2, out):
     nc = tc.nc
-    xf = x.flatten_outer_dims()
-    of = out.flatten_outer_dims()
+    frames = x.flatten_outer_dims()
+    rows = out.flatten_outer_dims()
 
     with ExitStack() as ctx:
-        const = ctx.enter_context(tc.tile_pool(name="const", bufs=1))
-        xtp = ctx.enter_context(tc.tile_pool(name="xtp", bufs=7))
-        qp = ctx.enter_context(tc.tile_pool(name="qp", bufs=3))
-        hbp = ctx.enter_context(tc.tile_pool(name="hbp", bufs=3))
-        ep = ctx.enter_context(tc.tile_pool(name="ep", bufs=6))
-        prp = ctx.enter_context(tc.tile_pool(name="prp", bufs=3))
-        smp = ctx.enter_context(tc.tile_pool(name="smp", bufs=2))
-        psx = ctx.enter_context(tc.psum_pool(name="psx", bufs=1))
-        psh = ctx.enter_context(tc.psum_pool(name="psh", bufs=2))
-        psa = ctx.enter_context(tc.psum_pool(name="psa", bufs=3))
-        psr = ctx.enter_context(tc.psum_pool(name="psr", bufs=2))
+        keep = ctx.enter_context(tc.tile_pool(name="keep", bufs=1))
+        xt_pool = ctx.enter_context(tc.tile_pool(name="xt_pool", bufs=7))
+        mx_pool = ctx.enter_context(tc.tile_pool(name="mx_pool", bufs=3))
+        h_pool = ctx.enter_context(tc.tile_pool(name="h_pool", bufs=3))
+        e_pool = ctx.enter_context(tc.tile_pool(name="e_pool", bufs=6))
+        prod_pool = ctx.enter_context(tc.tile_pool(name="prod_pool", bufs=3))
+        last_pool = ctx.enter_context(tc.tile_pool(name="last_pool", bufs=2))
+        x_banks = ctx.enter_context(tc.psum_pool(name="x_banks", bufs=1))
+        h_banks = ctx.enter_context(tc.psum_pool(name="h_banks", bufs=2))
+        a_banks = ctx.enter_context(tc.psum_pool(name="a_banks", bufs=3))
+        sum_banks = ctx.enter_context(tc.psum_pool(name="sum_banks", bufs=2))
         ctx.enter_context(tc.manual_schedule())
 
-        identb = const.tile([P, P], BF16)
-        make_identity(nc, identb[:])
-        identf = const.tile([P, P], F32)
-        make_identity(nc, identf[:])
+        ident_bf16 = keep.tile([P, P], BF16)
+        make_identity(nc, ident_bf16[:])
+        ident_f32 = keep.tile([P, P], F32)
+        make_identity(nc, ident_f32[:])
 
-        xs_tiles = []
-        for h in range(NH):
-            x_sb = const.tile([P, 8, P], BF16, name="x_sb%d" % h)
-            xs_tiles.append(x_sb)
+        x_tiles = []
+        for s in range(SLABS):
+            x_sb = keep.tile([P, FRAMES // P, P], BF16, name="x_sb%d" % s)
+            x_tiles.append(x_sb)
 
-        def load_x(h):
-            for j in range(8):
-                r0 = h * FR + j * P
-                nc.sync.dma_start(out=xs_tiles[h][:, j, :], in_=xf[r0 : r0 + P, :])
+        def load_x(s):
+            for j in range(FRAMES // P):
+                first = s * FRAMES + j * P
+                nc.sync.dma_start(out=x_tiles[s][:, j, :], in_=frames[first : first + P, :])
 
-        w1r = const.tile([P, 4, 512], BF16)
-        w2r = const.tile([P, 4, 512], BF16)
-        nc.sync.dma_start(out=w1r[:], in_=w1.rearrange("(p j) f -> p j f", j=4))
+        w1_rows = keep.tile([P, PACK, 512], BF16)
+        w2_rows = keep.tile([P, PACK, 512], BF16)
+        nc.sync.dma_start(out=w1_rows[:], in_=w1.rearrange("(p j) f -> p j f", j=PACK))
         load_x(0)
         load_x(1)
-        nc.sync.dma_start(out=w2r[:], in_=w2.rearrange("(p j) f -> p j f", j=4))
-        for h in range(2, NH):
-            load_x(h)
+        nc.sync.dma_start(out=w2_rows[:], in_=w2.rearrange("(p j) f -> p j f", j=PACK))
+        for s in range(2, SLABS):
+            load_x(s)
 
-        w1g = const.tile([P, 4, P, 4], BF16, align_bytes=64)
-        w2g = const.tile([P, 4, P, 4], BF16, align_bytes=64)
-        w1q = const.tile([P, 512], U32, align_bytes=64)
-        w1s = const.tile([P, 512], U8, align_bytes=64)
-        w2q = const.tile([P, 512], U32, align_bytes=64)
-        w2s = const.tile([P, 512], U8, align_bytes=64)
-        w1v = w1r[:].rearrange("p j (q t) -> p t q j", t=4)
-        nc.vector.tensor_copy(out=w1g[:, 0:2, :, :], in_=w1v[:, 0:2, :, :])
-        nc.scalar.copy(out=w1g[:, 2:4, :, :], in_=w1v[:, 2:4, :, :])
-        nc.scalar.copy(out=w2g[:], in_=w2r[:].rearrange("p j (q t) -> p t q j", t=4))
+        w1_grouped = keep.tile([P, PACK, P, PACK], BF16, align_bytes=64)
+        w2_grouped = keep.tile([P, PACK, P, PACK], BF16, align_bytes=64)
+        w1_codes = keep.tile([P, 512], U32, align_bytes=64)
+        w1_scales = keep.tile([P, 512], U8, align_bytes=64)
+        w2_codes = keep.tile([P, 512], U32, align_bytes=64)
+        w2_scales = keep.tile([P, 512], U8, align_bytes=64)
+        w1_view = w1_rows[:].rearrange("p j (q t) -> p t q j", t=PACK)
+        nc.vector.tensor_copy(out=w1_grouped[:, 0:2, :, :], in_=w1_view[:, 0:2, :, :])
+        nc.scalar.copy(out=w1_grouped[:, 2:4, :, :], in_=w1_view[:, 2:4, :, :])
+        nc.scalar.copy(out=w2_grouped[:], in_=w2_rows[:].rearrange("p j (q t) -> p t q j", t=PACK))
 
-        def quant_w(wq, ws, wg):
+        def quantise_weights(codes, scales, grouped):
             nc.vector.quantize_mx(
-                out=wq[:].bitcast(FP8X4),
-                scales=ws[:],
-                in_=wg[:].rearrange("p t q j -> p (t q j)"),
+                out=codes[:].bitcast(FP8X4),
+                scales=scales[:],
+                in_=grouped[:].rearrange("p t q j -> p (t q j)"),
             )
 
-        sn_tiles = []
-        for i, (h0, h1) in enumerate(PHASES):
-            sn = const.tile([P, 2, 2 * (h1 - h0), P], F32, name="sn%d" % i)
-            sn_tiles.append(sn)
+        sums_tiles = []
+        for g, (s0, s1) in enumerate(GROUPS):
+            sums_sb = keep.tile([P, 2, HALVES * (s1 - s0), P], F32, name="sums_sb%d" % g)
+            sums_tiles.append(sums_sb)
 
-        def phase_of(h):
-            for i, (h0, h1) in enumerate(PHASES):
-                if h0 <= h < h1:
-                    return i, h - h0
-            raise ValueError("no phase")
+        live = {}
 
-        st = {}
+        def transpose_x(s):
+            xt_ps = x_banks.tile([P, FRAMES], BF16)
+            for j in range(FRAMES // P):
+                nc.tensor.transpose(xt_ps[:, j * P : (j + 1) * P], x_tiles[s][:, j, :], ident_bf16[:])
+            live["xt_ps", s] = xt_ps
 
-        def xpose(h):
-            xb = psx.tile([P, FR], BF16)
-            for j in range(8):
-                nc.tensor.transpose(xb[:, j * P : (j + 1) * P], xs_tiles[h][:, j, :], identb[:])
-            st["xb", h] = xb
+        def copy_x(s):
+            xt = xt_pool.tile([P, FRAMES], BF16, align_bytes=64)
+            nc.vector.tensor_copy(out=xt[:], in_=live["xt_ps", s][:])
+            live["xt", s] = xt
 
-        def evacx(h):
-            xt = xtp.tile([P, FR], BF16, align_bytes=64)
-            nc.vector.tensor_copy(out=xt[:], in_=st["xb", h][:])
-            st["xt", h] = xt
+        def quantise_x(s):
+            x_codes = mx_pool.tile([P, WIN], U32, align_bytes=64)
+            x_scales = mx_pool.tile([P, WIN], U8, align_bytes=64)
+            nc.vector.quantize_mx(out=x_codes[:].bitcast(FP8X4), scales=x_scales[:], in_=live["xt", s][:])
+            live["x_mx", s] = (x_codes, x_scales)
 
-        def quantx(h):
-            xq = qp.tile([P, TOK], U32, align_bytes=64)
-            xsc = qp.tile([P, TOK], U8, align_bytes=64)
-            nc.vector.quantize_mx(out=xq[:].bitcast(FP8X4), scales=xsc[:], in_=st["xt", h][:])
-            st["xq", h] = (xq, xsc)
-
-        def mm1(h):
-            xq, xsc = st["xq", h]
-            for s in range(2):
-                hp = psh.tile([P, 4, P], F32)
-                for t in range(4):
+        def first_matmul(s):
+            x_codes, x_scales = live["x_mx", s]
+            for i in range(HALVES):
+                h_ps = h_banks.tile([P, PACK, P], F32)
+                for t in range(PACK):
                     nc.tensor.matmul_mx(
-                        out=hp[:, t, :],
-                        lhsT=w1q[:, t * P : (t + 1) * P].bitcast(FP8X4),
-                        lhsT_scale=w1s[:, t * P : (t + 1) * P],
-                        rhs=xq[:, s * P : (s + 1) * P].bitcast(FP8X4),
-                        rhs_scale=xsc[:, s * P : (s + 1) * P],
+                        out=h_ps[:, t, :],
+                        lhsT=w1_codes[:, t * P : (t + 1) * P].bitcast(FP8X4),
+                        lhsT_scale=w1_scales[:, t * P : (t + 1) * P],
+                        rhs=x_codes[:, i * P : (i + 1) * P].bitcast(FP8X4),
+                        rhs_scale=x_scales[:, i * P : (i + 1) * P],
                         start=True,
                         stop=True,
                     )
-                st["hp", h, s] = hp
+                live["h_ps", s, i] = h_ps
 
-        def relu(h):
-            hb = hbp.tile([P, TOK, 4], BF16, align_bytes=64)
-            nc.vector.tensor_scalar_max(
-                out=hb[:, 0:P, :], in0=st["hp", h, 0][:].rearrange("p t r -> p r t"), scalar1=0.0
-            )
-            st["hb", h] = hb
+        def relu_on_vector(s, halves):
+            if ("h", s) not in live:
+                h_bf16 = h_pool.tile([P, WIN, PACK], BF16, align_bytes=64)
+                live["h", s] = h_bf16
+            for i in halves:
+                nc.vector.tensor_scalar_max(
+                    out=live["h", s][:, i * P : (i + 1) * P, :],
+                    in0=live["h_ps", s, i][:].rearrange("p t r -> p r t"),
+                    scalar1=0.0,
+                )
 
-        def relu_act(h):
+        def relu_on_scalar(s, i):
             nc.scalar.activation(
-                out=st["hb", h][:, P : 2 * P, :],
-                in_=st["hp", h, 1][:].rearrange("p t r -> p r t"),
+                out=live["h", s][:, i * P : (i + 1) * P, :],
+                in_=live["h_ps", s, i][:].rearrange("p t r -> p r t"),
                 func=ACT.Relu,
             )
 
-        def quanth(h):
-            hq = qp.tile([P, TOK], U32, align_bytes=64)
-            hsc = qp.tile([P, TOK], U8, align_bytes=64)
+        def quantise_h(s):
+            h_codes = mx_pool.tile([P, WIN], U32, align_bytes=64)
+            h_scales = mx_pool.tile([P, WIN], U8, align_bytes=64)
             nc.vector.quantize_mx(
-                out=hq[:].bitcast(FP8X4),
-                scales=hsc[:],
-                in_=st["hb", h][:].rearrange("p r t -> p (r t)"),
+                out=h_codes[:].bitcast(FP8X4),
+                scales=h_scales[:],
+                in_=live["h", s][:].rearrange("p r t -> p (r t)"),
             )
-            st["hq", h] = (hq, hsc)
+            live["h_mx", s] = (h_codes, h_scales)
 
-        def mm2(h):
-            hq, hsc = st["hq", h]
+        def second_matmul(s):
+            h_codes, h_scales = live["h_mx", s]
             for u in range(2):
-                ap_ = psa.tile([P, 2, TOK], F32, name="a_ps")
+                a_ps = a_banks.tile([P, 2, WIN], F32)
                 for v in range(2):
                     m = 2 * u + v
                     nc.tensor.matmul_mx(
-                        out=ap_[:, v, :],
-                        lhsT=w2q[:, m * P : (m + 1) * P].bitcast(FP8X4),
-                        lhsT_scale=w2s[:, m * P : (m + 1) * P],
-                        rhs=hq[:].bitcast(FP8X4),
-                        rhs_scale=hsc[:],
+                        out=a_ps[:, v, :],
+                        lhsT=w2_codes[:, m * P : (m + 1) * P].bitcast(FP8X4),
+                        lhsT_scale=w2_scales[:, m * P : (m + 1) * P],
+                        rhs=h_codes[:].bitcast(FP8X4),
+                        rhs_scale=h_scales[:],
                         start=True,
                         stop=True,
                     )
-                st["a", h, u] = ap_
+                live["a_ps", s, u] = a_ps
 
-        def tanh_(h):
-            e = ep.tile([P, 4, TOK], F32)
+        def tanh(s):
+            e = e_pool.tile([P, PACK, WIN], F32)
             for u in range(2):
                 nc.scalar.activation(
-                    out=e[:, 2 * u : 2 * u + 2, :], in_=st["a", h, u][:], func=ACT.Tanh, scale=0.5
+                    out=e[:, 2 * u : 2 * u + 2, :], in_=live["a_ps", s, u][:], func=ACT.Tanh, scale=0.5
                 )
-            st["e", h] = e
+            live["e", s] = e
 
-        def exp_(h):
-            e = st["e", h]
+        def exp(s):
+            e = live["e", s]
             nc.scalar.activation(out=e[:], in_=e[:], func=ACT.Exp, scale=0.5)
 
-        def mult(h):
-            pr = prp.tile([P, 4, TOK], F32)
-            nc.vector.tensor_tensor(
-                out=pr[:],
-                in0=st["e", h][:],
-                in1=st["xt", h][:].rearrange("p (r m) -> p m r", m=4),
-                op=ALU.mult,
-            )
-            st["pr", h] = pr
+        def add_pairs(s):
+            e = live["e", s]
+            e_pairs = prod_pool.tile([P, 2, WIN], F32)
+            nc.vector.tensor_add(out=e_pairs[:], in0=e[:, 0:2, :], in1=e[:, 2:4, :])
+            live["e_pairs", s] = e_pairs
 
-        def pre(h):
-            e = st["e", h]
-            s2 = prp.tile([P, 2, TOK], F32)
-            nc.vector.tensor_add(out=s2[:], in0=e[:, 0:2, :], in1=e[:, 2:4, :])
-            st["s2", h] = s2
+        def multiply_by_x(s):
+            xe = prod_pool.tile([P, PACK, WIN], F32)
+            nc.vector.tensor_tensor(
+                out=xe[:],
+                in0=live["e", s][:],
+                in1=live["xt", s][:].rearrange("p (r m) -> p m r", m=PACK),
+                op=mybir.AluOpType.mult,
+            )
+            live["xe", s] = xe
 
         def add_up(dst, parts):
-            n = len(parts)
             for k, part in enumerate(parts):
                 nc.tensor.matmul(
-                    out=dst, lhsT=part, rhs=identf[:], is_transpose=True, start=(k == 0), stop=(k == n - 1)
+                    out=dst,
+                    lhsT=part,
+                    rhs=ident_f32[:],
+                    is_transpose=True,
+                    start=(k == 0),
+                    stop=(k == len(parts) - 1),
                 )
 
-        def reduce_first(h):
-            rp = psr.tile([P, 2, 2, P], F32)
-            st["rp", h] = rp
-            add_up(rp[:, 0, 0, :], [st["s2", h][:, k, 0:P] for k in range(2)])
+        def sums_first_part(s):
+            sums_ps = sum_banks.tile([P, 2, HALVES, P], F32)
+            live["sums_ps", s] = sums_ps
+            add_up(sums_ps[:, 0, 0, :], [live["e_pairs", s][:, k, 0:P] for k in range(2)])
 
-        def reduce_rest(h):
-            rp = st["rp", h]
-            add_up(rp[:, 0, 1, :], [st["s2", h][:, k, P : 2 * P] for k in range(2)])
-            for s in range(2):
-                add_up(rp[:, 1, s, :], [st["pr", h][:, m, s * P : (s + 1) * P] for m in range(4)])
+        def sums_second_part(s):
+            sums_ps = live["sums_ps", s]
+            add_up(sums_ps[:, 0, 1, :], [live["e_pairs", s][:, k, P : 2 * P] for k in range(2)])
+            for i in range(HALVES):
+                add_up(sums_ps[:, 1, i, :], [live["xe", s][:, m, i * P : (i + 1) * P] for m in range(PACK)])
 
-        def evacr(h):
-            i, k = phase_of(h)
-            nc.scalar.copy(out=sn_tiles[i][:, :, 2 * k : 2 * k + 2, :], in_=st["rp", h][:])
+        def place_of(s):
+            for g, (s0, s1) in enumerate(GROUPS):
+                if s0 <= s < s1:
+                    return sums_tiles[g][:, :, HALVES * (s - s0) : HALVES * (s - s0 + 1), :]
+            raise ValueError("slab %d is divided on Vector" % s)
 
-        def direct(h):
-            rp = st["rp", h]
-            rc = smp.tile([P, 2, P], F32)
-            nc.vector.reciprocal(out=rc[:], in_=rp[:, 0, :, :])
-            ot = smp.tile([P, 2, P], F32)
-            nc.vector.tensor_mul(out=ot[:], in0=rp[:, 1, :, :], in1=rc[:])
+        def store(s0, s1, result):
             nc.sync.dma_start(
-                out=of[h * TOK : (h + 1) * TOK, :].rearrange("(n p) c -> p n c", p=P), in_=ot[:]
+                out=rows[s0 * WIN : s1 * WIN, :].rearrange("(n p) c -> p n c", p=P), in_=result
             )
 
-        def ln_(i, k0, k1):
-            s_ = sn_tiles[i][:, 0, 2 * k0 : 2 * k1, :]
-            nc.scalar.activation(out=s_, in_=s_, func=ACT.Ln)
+        def sums_out(s):
+            if s >= BY_RECIPROCAL:
+                sums_ps = live["sums_ps", s]
+                inverse = last_pool.tile([P, HALVES, P], F32)
+                nc.vector.reciprocal(out=inverse[:], in_=sums_ps[:, 0, :, :])
+                result = last_pool.tile([P, HALVES, P], F32)
+                nc.vector.tensor_mul(out=result[:], in0=sums_ps[:, 1, :, :], in1=inverse[:])
+                store(s, s + 1, result[:])
+            elif within(s, SUMS_OUT_ON_VECTOR):
+                nc.vector.tensor_copy(out=place_of(s), in_=live["sums_ps", s][:])
+            else:
+                nc.scalar.copy(out=place_of(s), in_=live["sums_ps", s][:])
 
-        def rexp(i, k0, k1):
-            s_ = sn_tiles[i][:, 0, 2 * k0 : 2 * k1, :]
-            nc.scalar.activation(out=s_, in_=s_, func=ACT.Exp, scale=-1.0)
+        def ln(g):
+            nc.scalar.activation(out=sums_tiles[g][:, 0, :, :], in_=sums_tiles[g][:, 0, :, :], func=ACT.Ln)
 
-        def finish(i, k0, k1):
-            s_ = sn_tiles[i][:, 0, 2 * k0 : 2 * k1, :]
-            n_ = sn_tiles[i][:, 1, 2 * k0 : 2 * k1, :]
-            nc.vector.tensor_mul(out=n_, in0=n_, in1=s_)
-            r0 = (PHASES[i][0] + k0) * TOK
-            r1 = (PHASES[i][0] + k1) * TOK
-            nc.sync.dma_start(out=of[r0:r1, :].rearrange("(n p) c -> p n c", p=P), in_=n_)
+        def exp_of_minus(g):
+            nc.scalar.activation(
+                out=sums_tiles[g][:, 0, :, :], in_=sums_tiles[g][:, 0, :, :], func=ACT.Exp, scale=-1.0
+            )
 
-        NPER = NH + 9
-        act_slot = [[] for t in range(NPER + 8)]
-        dve_slot = [[] for t in range(NPER + 8)]
-        t0 = MID_CHUNKS[-1][1] - 1 + 6
-        for i, (h0, h1) in enumerate(MID_CHUNKS):
-            act_slot[t0].append((ln_, i, 0, h1 - h0))
-            act_slot[t0 + 1 + i].append((rexp, i, 0, h1 - h0))
-            dve_slot[t0 + 2 + i].append((finish, i, 0, h1 - h0))
-        tl = N_ACT - 1 + 6
-        for j, (h0, h1) in enumerate(END_CHUNKS):
-            act_slot[tl].append((ln_, len(MID_CHUNKS) + j, 0, h1 - h0))
-        for j, (h0, h1) in enumerate(END_CHUNKS):
-            act_slot[tl].append((rexp, len(MID_CHUNKS) + j, 0, h1 - h0))
-            dve_slot[tl + 2].append((finish, len(MID_CHUNKS) + j, 0, h1 - h0))
+        def finish(g):
+            nc.vector.tensor_mul(
+                out=sums_tiles[g][:, 1, :, :], in0=sums_tiles[g][:, 1, :, :], in1=sums_tiles[g][:, 0, :, :]
+            )
+            store(GROUPS[g][0], GROUPS[g][1], sums_tiles[g][:, 1, :, :])
 
-        def on(h):
-            return 0 <= h < NH
+        scalar_extra = [[] for t in range(STEPS)]
+        vector_extra = [[] for t in range(STEPS)]
+        for g in range(len(FIRST_LN)):
+            scalar_extra[STEP_LN1].append((ln, g))
+            scalar_extra[STEP_LN1 + 1 + g].append((exp_of_minus, g))
+            vector_extra[STEP_LN1 + 2 + g].append((finish, g))
+        for g in range(len(FIRST_LN), len(GROUPS)):
+            scalar_extra[STEP_LN2].append((ln, g))
+        for g in range(len(FIRST_LN), len(GROUPS)):
+            scalar_extra[STEP_LN2].append((exp_of_minus, g))
+            vector_extra[STEP_LN2 + 2].append((finish, g))
 
-        for t in range(NPER):
-            if on(t):
-                xpose(t)
-            if on(t - 5):
-                reduce_first(t - 5)
-            if on(t - 1):
-                mm1(t - 1)
-            if on(t - 2):
-                quanth(t - 2)
-            if on(t - 5):
-                reduce_rest(t - 5)
-            if on(t):
-                evacx(t)
+        def on(s):
+            return 0 <= s < SLABS
+
+        for t in range(STEPS):
+            if on(t - LAG_X):
+                transpose_x(t - LAG_X)
+            if on(t - LAG_SUMS):
+                sums_first_part(t - LAG_SUMS)
+            if on(t - LAG_MM1):
+                first_matmul(t - LAG_MM1)
+            if on(t - LAG_MM2):
+                quantise_h(t - LAG_MM2)
+            if on(t - LAG_SUMS):
+                sums_second_part(t - LAG_SUMS)
+            if on(t - LAG_X):
+                copy_x(t - LAG_X)
             if t == 0:
-                quant_w(w1q, w1s, w1g)
-            if on(t - 4):
-                pre(t - 4)
-            if on(t):
-                quantx(t)
-            if on(t - 1):
-                relu(t - 1)
+                quantise_weights(w1_codes, w1_scales, w1_grouped)
+            if on(t - LAG_PROD):
+                add_pairs(t - LAG_PROD)
+            if on(t - LAG_X):
+                quantise_x(t - LAG_X)
+            if on(t - LAG_MM1):
+                relu_on_vector(t - LAG_MM1, (0, 1) if within(t - LAG_MM1, RELU_ALL_ON_VECTOR) else (0,))
             if t == 1:
-                quant_w(w2q, w2s, w2g)
-            if on(t - 2):
-                mm2(t - 2)
-            if on(t - 1):
-                relu_act(t - 1)
-            if on(t - 3):
-                exp_(t - 3)
-            if on(t - 4):
-                mult(t - 4)
-            for f, i, k0, k1 in dve_slot[t]:
-                f(i, k0, k1)
-            for f, i, k0, k1 in act_slot[t]:
-                f(i, k0, k1)
-            if on(t - 5):
-                if t - 5 < N_ACT:
-                    evacr(t - 5)
-                else:
-                    direct(t - 5)
-            if on(t - 2):
-                tanh_(t - 2)
+                quantise_weights(w2_codes, w2_scales, w2_grouped)
+            if on(t - LAG_MM2):
+                second_matmul(t - LAG_MM2)
+            if on(t - LAG_MM1) and not within(t - LAG_MM1, RELU_ALL_ON_VECTOR):
+                relu_on_scalar(t - LAG_MM1, 1)
+            if on(t - LAG_EXP):
+                exp(t - LAG_EXP)
+            if on(t - LAG_PROD):
+                multiply_by_x(t - LAG_PROD)
+            for work, g in vector_extra[t]:
+                work(g)
+            for work, g in scalar_extra[t]:
+                work(g)
+            if on(t - LAG_SUMS):
+                sums_out(t - LAG_SUMS)
+            if on(t - LAG_MM2):
+                tanh(t - LAG_MM2)

@@ -18,6 +18,7 @@ SLABS = 32
 WIN = 256
 FRAMES = WIN * PACK
 HALVES = WIN // P
+BY_PRODUCT = 6
 
 LAG_X = 0
 LAG_MM1 = 1
@@ -114,7 +115,16 @@ def tile_dwamformer_pa_t_kernel(tc, x, w1, w2, out):
         def transpose_x(s):
             xt_ps = x_banks.tile([P, FRAMES], BF16)
             for j in range(FRAMES // P):
-                nc.tensor.transpose(xt_ps[:, j * P : (j + 1) * P], x_tiles[s][:, j, :], ident_bf16[:])
+                if j < BY_PRODUCT:
+                    nc.tensor.matmul(
+                        out=xt_ps[:, j * P : (j + 1) * P],
+                        lhsT=x_tiles[s][:, j, :],
+                        rhs=ident_bf16[:],
+                        start=True,
+                        stop=True,
+                    )
+                else:
+                    nc.tensor.transpose(xt_ps[:, j * P : (j + 1) * P], x_tiles[s][:, j, :], ident_bf16[:])
             live["xt_ps", s] = xt_ps
 
         def copy_x(s):

@@ -21,11 +21,12 @@ HALVES = WIN // P
 BY_PRODUCT = 6
 
 LAG_X = 0
-LAG_MM1 = 1
-LAG_MM2 = 2
-LAG_EXP = 3
-LAG_PROD = 4
-LAG_SUMS = 5
+LAG_QX = 1
+LAG_MM1 = 2
+LAG_MM2 = 3
+LAG_EXP = 4
+LAG_PROD = 5
+LAG_SUMS = 6
 
 FIRST_LN = ((0, 3), (3, 6), (6, 9), (9, 12), (12, 15), (15, 18), (18, 21))
 SECOND_LN = ((21, 24), (24, 27), (27, 30))
@@ -57,9 +58,9 @@ def tile_dwamformer_pa_t_kernel(tc, x, w1, w2, out):
         e_pool = ctx.enter_context(tc.tile_pool(name="e_pool", bufs=6))
         prod_pool = ctx.enter_context(tc.tile_pool(name="prod_pool", bufs=3))
         last_pool = ctx.enter_context(tc.tile_pool(name="last_pool", bufs=2))
-        x_banks = ctx.enter_context(tc.psum_pool(name="x_banks", bufs=1))
+        x_banks = ctx.enter_context(tc.psum_pool(name="x_banks", bufs=2))
         h_banks = ctx.enter_context(tc.psum_pool(name="h_banks", bufs=2))
-        a_banks = ctx.enter_context(tc.psum_pool(name="a_banks", bufs=3))
+        a_banks = ctx.enter_context(tc.psum_pool(name="a_banks", bufs=2))
         sum_banks = ctx.enter_context(tc.psum_pool(name="sum_banks", bufs=2))
         ctx.enter_context(tc.manual_schedule())
 
@@ -238,16 +239,13 @@ def tile_dwamformer_pa_t_kernel(tc, x, w1, w2, out):
                     stop=(k == len(parts) - 1),
                 )
 
-        def sums_first_part(s):
+        def sums(s):
             sums_ps = sum_banks.tile([P, 2, HALVES, P], F32)
             live["sums_ps", s] = sums_ps
-            add_up(sums_ps[:, 0, 0, :], [live["e_pairs", s][:, k, 0:P] for k in range(2)])
-
-        def sums_second_part(s):
-            sums_ps = live["sums_ps", s]
-            add_up(sums_ps[:, 0, 1, :], [live["e_pairs", s][:, k, P : 2 * P] for k in range(2)])
             for i in range(HALVES):
                 add_up(sums_ps[:, 1, i, :], [live["xe", s][:, m, i * P : (i + 1) * P] for m in range(PACK)])
+            for i in range(HALVES):
+                add_up(sums_ps[:, 0, i, :], [live["e_pairs", s][:, k, i * P : (i + 1) * P] for k in range(2)])
 
         def place_of(s):
             for g, (s0, s1) in enumerate(GROUPS):
@@ -303,41 +301,37 @@ def tile_dwamformer_pa_t_kernel(tc, x, w1, w2, out):
             return 0 <= s < SLABS
 
         for t in range(STEPS):
-            if on(t - LAG_X):
-                transpose_x(t - LAG_X)
-            if on(t - LAG_SUMS):
-                sums_first_part(t - LAG_SUMS)
             if on(t - LAG_MM1):
                 first_matmul(t - LAG_MM1)
             if on(t - LAG_MM2):
-                quantise_h(t - LAG_MM2)
-            if on(t - LAG_SUMS):
-                sums_second_part(t - LAG_SUMS)
+                second_matmul(t - LAG_MM2)
             if on(t - LAG_X):
-                copy_x(t - LAG_X)
+                transpose_x(t - LAG_X)
             if t == 0:
                 quantise_weights(w1_codes, w1_scales, w1_grouped)
-            if on(t - LAG_PROD):
-                add_pairs(t - LAG_PROD)
-            if on(t - LAG_X):
-                quantise_x(t - LAG_X)
-            if on(t - LAG_MM1):
-                relu_on_vector(t - LAG_MM1, (0, 1) if within(t - LAG_MM1, RELU_ALL_ON_VECTOR) else (0,))
-            if t == 1:
-                quantise_weights(w2_codes, w2_scales, w2_grouped)
-            if on(t - LAG_MM2):
-                second_matmul(t - LAG_MM2)
-            if on(t - LAG_MM1) and not within(t - LAG_MM1, RELU_ALL_ON_VECTOR):
-                relu_on_scalar(t - LAG_MM1, 1)
-            if on(t - LAG_EXP):
-                exp(t - LAG_EXP)
+            if on(t - LAG_QX):
+                copy_x(t - LAG_QX)
             if on(t - LAG_PROD):
                 multiply_by_x(t - LAG_PROD)
+                add_pairs(t - LAG_PROD)
+                sums(t - LAG_PROD)
+            if on(t - LAG_MM1):
+                relu_on_vector(t - LAG_MM1, (0, 1) if within(t - LAG_MM1, RELU_ALL_ON_VECTOR) else (0,))
+            if on(t - LAG_QX):
+                quantise_x(t - LAG_QX)
+            if t == 1:
+                quantise_weights(w2_codes, w2_scales, w2_grouped)
+            if on(t - LAG_EXP):
+                exp(t - LAG_EXP)
+            if on(t - LAG_MM1) and not within(t - LAG_MM1, RELU_ALL_ON_VECTOR):
+                relu_on_scalar(t - LAG_MM1, 1)
             for work, g in vector_extra[t]:
                 work(g)
             for work, g in scalar_extra[t]:
                 work(g)
-            if on(t - LAG_SUMS):
-                sums_out(t - LAG_SUMS)
+            if on(t - LAG_MM1):
+                quantise_h(t - LAG_MM1)
             if on(t - LAG_MM2):
                 tanh(t - LAG_MM2)
+            if on(t - LAG_SUMS):
+                sums_out(t - LAG_SUMS)

@@ -20,25 +20,22 @@ FRAMES = WIN * PACK
 HALVES = WIN // P
 BY_PRODUCT = 6
 
-LAG_X = 0
-LAG_QX = 1
-LAG_MM1 = 2
-LAG_MM2 = 3
-LAG_EXP = 4
-LAG_PROD = 5
-LAG_SUMS = 6
+LEAD = 2
 
 FIRST_LN = ((0, 3), (3, 6), (6, 9), (9, 12), (12, 15), (15, 18), (18, 21))
 SECOND_LN = ((21, 24), (24, 27), (27, 30))
 GROUPS = FIRST_LN + SECOND_LN
 END_FIRST = 21
 BY_RECIPROCAL = 30
-STEP_LN1 = END_FIRST + LAG_SUMS
-STEP_LN2 = BY_RECIPROCAL + LAG_SUMS
-assert STEP_LN1 + len(FIRST_LN) == SLABS - 1 + LAG_MM2
-RELU_ALL_ON_VECTOR = (STEP_LN1 - 1 - LAG_MM1, STEP_LN1 + 2 - LAG_MM1)
-SUMS_OUT_ON_VECTOR = (STEP_LN1 - LAG_SUMS, STEP_LN1 + 4 - LAG_SUMS)
-STEPS = STEP_LN2 + 3
+LN_STEP = END_FIRST + 3 + LEAD
+PAUSE = 3
+STEPS = SLABS + 3 + LEAD + PAUSE
+
+
+def back_slab(t):
+    if t < LN_STEP:
+        return t - LEAD
+    return t - LEAD - PAUSE if t >= LN_STEP + PAUSE else None
 
 
 def within(s, span):
@@ -52,10 +49,10 @@ def tile_dwamformer_pa_t_kernel(tc, x, w1, w2, out):
 
     with ExitStack() as ctx:
         keep = ctx.enter_context(tc.tile_pool(name="keep", bufs=1))
-        xt_pool = ctx.enter_context(tc.tile_pool(name="xt_pool", bufs=7))
-        mx_pool = ctx.enter_context(tc.tile_pool(name="mx_pool", bufs=3))
-        h_pool = ctx.enter_context(tc.tile_pool(name="h_pool", bufs=3))
-        e_pool = ctx.enter_context(tc.tile_pool(name="e_pool", bufs=6))
+        xt_pool = ctx.enter_context(tc.tile_pool(name="xt_pool", bufs=9))
+        mx_pool = ctx.enter_context(tc.tile_pool(name="mx_pool", bufs=6))
+        h_pool = ctx.enter_context(tc.tile_pool(name="h_pool", bufs=4))
+        e_pool = ctx.enter_context(tc.tile_pool(name="e_pool", bufs=5))
         prod_pool = ctx.enter_context(tc.tile_pool(name="prod_pool", bufs=3))
         last_pool = ctx.enter_context(tc.tile_pool(name="last_pool", bufs=2))
         x_banks = ctx.enter_context(tc.psum_pool(name="x_banks", bufs=2))
@@ -83,9 +80,8 @@ def tile_dwamformer_pa_t_kernel(tc, x, w1, w2, out):
         w2_rows = keep.tile([P, PACK, 512], BF16)
         nc.sync.dma_start(out=w1_rows[:], in_=w1.rearrange("(p j) f -> p j f", j=PACK))
         load_x(0)
-        load_x(1)
         nc.sync.dma_start(out=w2_rows[:], in_=w2.rearrange("(p j) f -> p j f", j=PACK))
-        for s in range(2, SLABS):
+        for s in range(1, SLABS):
             load_x(s)
 
         w1_grouped = keep.tile([P, PACK, P, PACK], BF16, align_bytes=64)
@@ -95,8 +91,8 @@ def tile_dwamformer_pa_t_kernel(tc, x, w1, w2, out):
         w2_codes = keep.tile([P, 512], U32, align_bytes=64)
         w2_scales = keep.tile([P, 512], U8, align_bytes=64)
         w1_view = w1_rows[:].rearrange("p j (q t) -> p t q j", t=PACK)
-        nc.vector.tensor_copy(out=w1_grouped[:, 0:2, :, :], in_=w1_view[:, 0:2, :, :])
-        nc.scalar.copy(out=w1_grouped[:, 2:4, :, :], in_=w1_view[:, 2:4, :, :])
+        nc.vector.tensor_copy(out=w1_grouped[:, 0:3, :, :], in_=w1_view[:, 0:3, :, :])
+        nc.scalar.copy(out=w1_grouped[:, 3:4, :, :], in_=w1_view[:, 3:4, :, :])
         nc.scalar.copy(out=w2_grouped[:], in_=w2_rows[:].rearrange("p j (q t) -> p t q j", t=PACK))
 
         def quantise_weights(codes, scales, grouped):
@@ -245,7 +241,7 @@ def tile_dwamformer_pa_t_kernel(tc, x, w1, w2, out):
             for i in range(HALVES):
                 add_up(sums_ps[:, 1, i, :], [live["xe", s][:, m, i * P : (i + 1) * P] for m in range(PACK)])
             for i in range(HALVES):
-                add_up(sums_ps[:, 0, i, :], [live["e_pairs", s][:, k, i * P : (i + 1) * P] for k in range(2)])
+                add_up(sums_ps[:, 0, i, :], [live["e", s][:, m, i * P : (i + 1) * P] for m in range(PACK)])
 
         def place_of(s):
             for g, (s0, s1) in enumerate(GROUPS):
@@ -266,7 +262,7 @@ def tile_dwamformer_pa_t_kernel(tc, x, w1, w2, out):
                 result = last_pool.tile([P, HALVES, P], F32)
                 nc.vector.tensor_mul(out=result[:], in0=sums_ps[:, 1, :, :], in1=inverse[:])
                 store(s, s + 1, result[:])
-            elif within(s, SUMS_OUT_ON_VECTOR):
+            elif s % 3 == 0 or s >= END_FIRST:
                 nc.vector.tensor_copy(out=place_of(s), in_=live["sums_ps", s][:])
             else:
                 nc.scalar.copy(out=place_of(s), in_=live["sums_ps", s][:])
@@ -285,53 +281,57 @@ def tile_dwamformer_pa_t_kernel(tc, x, w1, w2, out):
             )
             store(GROUPS[g][0], GROUPS[g][1], sums_tiles[g][:, 1, :, :])
 
-        scalar_extra = [[] for t in range(STEPS)]
-        vector_extra = [[] for t in range(STEPS)]
+        scalar_extra = [[] for t in range(STEPS + 1)]
+        vector_extra = [[] for t in range(STEPS + 1)]
         for g in range(len(FIRST_LN)):
-            scalar_extra[STEP_LN1].append((ln, g))
-            scalar_extra[STEP_LN1 + 1 + g].append((exp_of_minus, g))
-            vector_extra[STEP_LN1 + 2 + g].append((finish, g))
+            scalar_extra[LN_STEP].append((ln, g))
+            scalar_extra[LN_STEP + PAUSE + g].append((exp_of_minus, g))
+            vector_extra[LN_STEP + PAUSE + 1 + g].append((finish, g))
         for g in range(len(FIRST_LN), len(GROUPS)):
-            scalar_extra[STEP_LN2].append((ln, g))
+            scalar_extra[STEPS - 1].append((ln, g))
         for g in range(len(FIRST_LN), len(GROUPS)):
-            scalar_extra[STEP_LN2].append((exp_of_minus, g))
-            vector_extra[STEP_LN2 + 2].append((finish, g))
+            scalar_extra[STEPS - 1].append((exp_of_minus, g))
+            vector_extra[STEPS].append((finish, g))
 
         def on(s):
-            return 0 <= s < SLABS
+            return s is not None and 0 <= s < SLABS
 
-        for t in range(STEPS):
-            if on(t - LAG_MM1):
-                first_matmul(t - LAG_MM1)
-            if on(t - LAG_MM2):
-                second_matmul(t - LAG_MM2)
-            if on(t - LAG_X):
-                transpose_x(t - LAG_X)
+        transpose_x(0)
+        for t in range(STEPS + 1):
+            f = t
+            b = back_slab(t)
+            c = [None if b is None else b - k for k in range(4)]
+            relu_all = t >= LN_STEP
+            if on(f - 1):
+                first_matmul(f - 1)
+            if on(c[0]):
+                second_matmul(c[0])
+            if on(f + 1):
+                transpose_x(f + 1)
             if t == 0:
                 quantise_weights(w1_codes, w1_scales, w1_grouped)
-            if on(t - LAG_QX):
-                copy_x(t - LAG_QX)
-            if on(t - LAG_PROD):
-                multiply_by_x(t - LAG_PROD)
-                add_pairs(t - LAG_PROD)
-                sums(t - LAG_PROD)
-            if on(t - LAG_MM1):
-                relu_on_vector(t - LAG_MM1, (0, 1) if within(t - LAG_MM1, RELU_ALL_ON_VECTOR) else (0,))
-            if on(t - LAG_QX):
-                quantise_x(t - LAG_QX)
+            if on(f):
+                copy_x(f)
+            if on(c[2]):
+                multiply_by_x(c[2])
+                sums(c[2])
+            if on(f - 1):
+                relu_on_vector(f - 1, (0, 1) if relu_all else (0,))
+            if on(f):
+                quantise_x(f)
             if t == 1:
                 quantise_weights(w2_codes, w2_scales, w2_grouped)
-            if on(t - LAG_EXP):
-                exp(t - LAG_EXP)
-            if on(t - LAG_MM1) and not within(t - LAG_MM1, RELU_ALL_ON_VECTOR):
-                relu_on_scalar(t - LAG_MM1, 1)
-            for work, g in vector_extra[t]:
-                work(g)
             for work, g in scalar_extra[t]:
                 work(g)
-            if on(t - LAG_MM1):
-                quantise_h(t - LAG_MM1)
-            if on(t - LAG_MM2):
-                tanh(t - LAG_MM2)
-            if on(t - LAG_SUMS):
-                sums_out(t - LAG_SUMS)
+            if on(c[1]):
+                exp(c[1])
+            if on(f - 1) and not relu_all:
+                relu_on_scalar(f - 1, 1)
+            for work, g in vector_extra[t]:
+                work(g)
+            if on(f - 1):
+                quantise_h(f - 1)
+            if on(c[0]):
+                tanh(c[0])
+            if on(c[3]):
+                sums_out(c[3])

@@ -21,25 +21,13 @@ HALVES = WIN // P
 BY_PRODUCT = 6
 
 LEAD = 2
-
-FIRST_LN = ((0, 3), (3, 6), (6, 9), (9, 12), (12, 15), (15, 18), (18, 21))
-SECOND_LN = ((21, 24), (24, 27), (27, 30))
-GROUPS = FIRST_LN + SECOND_LN
-END_FIRST = 21
-BY_RECIPROCAL = 30
-LN_STEP = END_FIRST + 3 + LEAD
-PAUSE = 3
-STEPS = SLABS + 3 + LEAD + PAUSE
+EARLY = 4
+AHEAD = 6
+LN_SLABS = 4
 
 
-def back_slab(t):
-    if t < LN_STEP:
-        return t - LEAD
-    return t - LEAD - PAUSE if t >= LN_STEP + PAUSE else None
-
-
-def within(s, span):
-    return span[0] <= s < span[1]
+def left_for_the_end(s):
+    return s >= 4 and s % 2 == 1
 
 
 def tile_dwamformer_pa_t_kernel(tc, x, w1, w2, out):
@@ -49,12 +37,10 @@ def tile_dwamformer_pa_t_kernel(tc, x, w1, w2, out):
 
     with ExitStack() as ctx:
         keep = ctx.enter_context(tc.tile_pool(name="keep", bufs=1))
-        xt_pool = ctx.enter_context(tc.tile_pool(name="xt_pool", bufs=9))
-        mx_pool = ctx.enter_context(tc.tile_pool(name="mx_pool", bufs=6))
-        h_pool = ctx.enter_context(tc.tile_pool(name="h_pool", bufs=4))
-        e_pool = ctx.enter_context(tc.tile_pool(name="e_pool", bufs=5))
-        prod_pool = ctx.enter_context(tc.tile_pool(name="prod_pool", bufs=3))
-        last_pool = ctx.enter_context(tc.tile_pool(name="last_pool", bufs=2))
+        xt_pool = ctx.enter_context(tc.tile_pool(name="xt_pool", bufs=6))
+        mx_pool = ctx.enter_context(tc.tile_pool(name="mx_pool", bufs=4))
+        h_pool = ctx.enter_context(tc.tile_pool(name="h_pool", bufs=3))
+        x_pool = ctx.enter_context(tc.tile_pool(name="x_pool", bufs=8))
         x_banks = ctx.enter_context(tc.psum_pool(name="x_banks", bufs=2))
         h_banks = ctx.enter_context(tc.psum_pool(name="h_banks", bufs=2))
         a_banks = ctx.enter_context(tc.psum_pool(name="a_banks", bufs=2))
@@ -66,33 +52,32 @@ def tile_dwamformer_pa_t_kernel(tc, x, w1, w2, out):
         ident_f32 = keep.tile([P, P], F32)
         make_identity(nc, ident_f32[:])
 
-        x_tiles = []
-        for s in range(SLABS):
-            x_sb = keep.tile([P, FRAMES // P, P], BF16, name="x_sb%d" % s)
-            x_tiles.append(x_sb)
+        x_tiles = {}
 
         def load_x(s):
+            x_sb = x_pool.tile([P, FRAMES // P, P], BF16)
+            x_tiles[s] = x_sb
             for j in range(FRAMES // P):
                 first = s * FRAMES + j * P
                 nc.sync.dma_start(out=x_tiles[s][:, j, :], in_=frames[first : first + P, :])
 
-        w1_rows = keep.tile([P, PACK, 512], BF16)
-        w2_rows = keep.tile([P, PACK, 512], BF16)
+        w1_rows = keep.tile([P, PACK, 512], BF16, name="e_28", align_bytes=64)
+        w2_rows = keep.tile([P, PACK, 512], BF16, name="e_29", align_bytes=64)
         nc.sync.dma_start(out=w1_rows[:], in_=w1.rearrange("(p j) f -> p j f", j=PACK))
         load_x(0)
         nc.sync.dma_start(out=w2_rows[:], in_=w2.rearrange("(p j) f -> p j f", j=PACK))
-        for s in range(1, SLABS):
+        for s in range(1, AHEAD):
             load_x(s)
 
-        w1_grouped = keep.tile([P, PACK, P, PACK], BF16, align_bytes=64)
-        w2_grouped = keep.tile([P, PACK, P, PACK], BF16, align_bytes=64)
+        w1_grouped = keep.tile([P, PACK, P, PACK], BF16, name="e_30", align_bytes=64)
+        w2_grouped = keep.tile([P, PACK, P, PACK], BF16, name="e_31", align_bytes=64)
         w1_codes = keep.tile([P, 512], U32, align_bytes=64)
         w1_scales = keep.tile([P, 512], U8, align_bytes=64)
         w2_codes = keep.tile([P, 512], U32, align_bytes=64)
         w2_scales = keep.tile([P, 512], U8, align_bytes=64)
         w1_view = w1_rows[:].rearrange("p j (q t) -> p t q j", t=PACK)
-        nc.vector.tensor_copy(out=w1_grouped[:, 0:3, :, :], in_=w1_view[:, 0:3, :, :])
-        nc.scalar.copy(out=w1_grouped[:, 3:4, :, :], in_=w1_view[:, 3:4, :, :])
+        nc.vector.tensor_copy(out=w1_grouped[:, 0:2, :, :], in_=w1_view[:, 0:2, :, :])
+        nc.scalar.copy(out=w1_grouped[:, 2:4, :, :], in_=w1_view[:, 2:4, :, :])
         nc.scalar.copy(out=w2_grouped[:], in_=w2_rows[:].rearrange("p j (q t) -> p t q j", t=PACK))
 
         def quantise_weights(codes, scales, grouped):
@@ -102,15 +87,13 @@ def tile_dwamformer_pa_t_kernel(tc, x, w1, w2, out):
                 in_=grouped[:].rearrange("p t q j -> p (t q j)"),
             )
 
-        sums_tiles = []
-        for g, (s0, s1) in enumerate(GROUPS):
-            sums_sb = keep.tile([P, 2, HALVES * (s1 - s0), P], F32, name="sums_sb%d" % g)
-            sums_tiles.append(sums_sb)
+        s_all = keep.tile([P, SLABS * HALVES, P], F32)
+        n_early = keep.tile([P, EARLY * HALVES, P], F32)
 
         live = {}
 
         def transpose_x(s):
-            xt_ps = x_banks.tile([P, FRAMES], BF16)
+            xt_ps = x_banks.tile([P, FRAMES], BF16, name="xt_ps")
             for j in range(FRAMES // P):
                 if j < BY_PRODUCT:
                     nc.tensor.matmul(
@@ -125,7 +108,10 @@ def tile_dwamformer_pa_t_kernel(tc, x, w1, w2, out):
             live["xt_ps", s] = xt_ps
 
         def copy_x(s):
-            xt = xt_pool.tile([P, FRAMES], BF16, align_bytes=64)
+            if left_for_the_end(s):
+                xt = keep.tile([P, FRAMES], BF16, name="xt_%d" % s, align_bytes=64)
+            else:
+                xt = xt_pool.tile([P, FRAMES], BF16, align_bytes=64)
             nc.vector.tensor_copy(out=xt[:], in_=live["xt_ps", s][:])
             live["xt", s] = xt
 
@@ -138,7 +124,7 @@ def tile_dwamformer_pa_t_kernel(tc, x, w1, w2, out):
         def first_matmul(s):
             x_codes, x_scales = live["x_mx", s]
             for i in range(HALVES):
-                h_ps = h_banks.tile([P, PACK, P], F32)
+                h_ps = h_banks.tile([P, PACK, P], F32, name="h_ps")
                 for t in range(PACK):
                     nc.tensor.matmul_mx(
                         out=h_ps[:, t, :],
@@ -182,7 +168,7 @@ def tile_dwamformer_pa_t_kernel(tc, x, w1, w2, out):
         def second_matmul(s):
             h_codes, h_scales = live["h_mx", s]
             for u in range(2):
-                a_ps = a_banks.tile([P, 2, WIN], F32)
+                a_ps = a_banks.tile([P, 2, WIN], F32, name="a_ps")
                 for v in range(2):
                     m = 2 * u + v
                     nc.tensor.matmul_mx(
@@ -197,7 +183,7 @@ def tile_dwamformer_pa_t_kernel(tc, x, w1, w2, out):
                 live["a_ps", s, u] = a_ps
 
         def tanh(s):
-            e = e_pool.tile([P, PACK, WIN], F32)
+            e = keep.tile([P, PACK, WIN], F32, name="e_%d" % (s if s >= EARLY else s + EARLY), align_bytes=64)
             for u in range(2):
                 nc.scalar.activation(
                     out=e[:, 2 * u : 2 * u + 2, :], in_=live["a_ps", s, u][:], func=ACT.Tanh, scale=0.5
@@ -208,130 +194,156 @@ def tile_dwamformer_pa_t_kernel(tc, x, w1, w2, out):
             e = live["e", s]
             nc.scalar.activation(out=e[:], in_=e[:], func=ACT.Exp, scale=0.5)
 
-        def add_pairs(s):
-            e = live["e", s]
-            e_pairs = prod_pool.tile([P, 2, WIN], F32)
-            nc.vector.tensor_add(out=e_pairs[:], in0=e[:, 0:2, :], in1=e[:, 2:4, :])
-            live["e_pairs", s] = e_pairs
-
         def multiply_by_x(s):
-            xe = prod_pool.tile([P, PACK, WIN], F32)
+            e = live["e", s]
+            if s < EARLY:
+                xe = keep.tile([P, PACK, WIN], F32, name="e_%d" % (s + 2 * EARLY), align_bytes=64)
+            else:
+                xe = e
             nc.vector.tensor_tensor(
                 out=xe[:],
-                in0=live["e", s][:],
+                in0=e[:],
                 in1=live["xt", s][:].rearrange("p (r m) -> p m r", m=PACK),
                 op=mybir.AluOpType.mult,
             )
             live["xe", s] = xe
 
-        def add_up(dst, parts):
-            for k, part in enumerate(parts):
+        def add_up(dst, tile, i):
+            for m in range(PACK):
                 nc.tensor.matmul(
                     out=dst,
-                    lhsT=part,
+                    lhsT=tile[:, m, i * P : (i + 1) * P],
                     rhs=ident_f32[:],
                     is_transpose=True,
-                    start=(k == 0),
-                    stop=(k == len(parts) - 1),
+                    start=(m == 0),
+                    stop=(m == PACK - 1),
                 )
 
-        def sums(s):
-            sums_ps = sum_banks.tile([P, 2, HALVES, P], F32)
-            live["sums_ps", s] = sums_ps
+        def sum_e(s):
+            sums_ps = sum_banks.tile([P, PACK, P], F32, name="sums_ps")
+            live["s_ps", s] = sums_ps
             for i in range(HALVES):
-                add_up(sums_ps[:, 1, i, :], [live["xe", s][:, m, i * P : (i + 1) * P] for m in range(PACK)])
-            for i in range(HALVES):
-                add_up(sums_ps[:, 0, i, :], [live["e", s][:, m, i * P : (i + 1) * P] for m in range(PACK)])
+                add_up(sums_ps[:, i, :], live["e", s], i)
 
-        def place_of(s):
-            for g, (s0, s1) in enumerate(GROUPS):
-                if s0 <= s < s1:
-                    return sums_tiles[g][:, :, HALVES * (s - s0) : HALVES * (s - s0 + 1), :]
-            raise ValueError("slab %d is divided on Vector" % s)
+        def sum_xe(s):
+            sums_ps = sum_banks.tile([P, PACK, P], F32, name="sums_ps")
+            live["n_ps", s] = sums_ps
+            for i in range(HALVES):
+                add_up(sums_ps[:, i, :], live["xe", s], i)
+
+        def blocks(s0, s1):
+            return slice(HALVES * s0, HALVES * s1)
+
+        def s_out(s, on_vector):
+            dst, src = s_all[:, blocks(s, s + 1), :], live["s_ps", s][:, 0:HALVES, :]
+            if on_vector:
+                nc.vector.tensor_copy(out=dst, in_=src)
+            else:
+                nc.scalar.copy(out=dst, in_=src)
+
+        def n_out(s):
+            nc.scalar.copy(out=n_early[:, blocks(s, s + 1), :], in_=live["n_ps", s][:, 0:HALVES, :])
 
         def store(s0, s1, result):
             nc.sync.dma_start(
                 out=rows[s0 * WIN : s1 * WIN, :].rearrange("(n p) c -> p n c", p=P), in_=result
             )
 
-        def sums_out(s):
-            if s >= BY_RECIPROCAL:
-                sums_ps = live["sums_ps", s]
-                inverse = last_pool.tile([P, HALVES, P], F32)
-                nc.vector.reciprocal(out=inverse[:], in_=sums_ps[:, 0, :, :])
-                result = last_pool.tile([P, HALVES, P], F32)
-                nc.vector.tensor_mul(out=result[:], in0=sums_ps[:, 1, :, :], in1=inverse[:])
-                store(s, s + 1, result[:])
-            elif s % 3 == 0 or s >= END_FIRST:
-                nc.vector.tensor_copy(out=place_of(s), in_=live["sums_ps", s][:])
-            else:
-                nc.scalar.copy(out=place_of(s), in_=live["sums_ps", s][:])
-
-        def ln(g):
-            nc.scalar.activation(out=sums_tiles[g][:, 0, :, :], in_=sums_tiles[g][:, 0, :, :], func=ACT.Ln)
-
-        def exp_of_minus(g):
-            nc.scalar.activation(
-                out=sums_tiles[g][:, 0, :, :], in_=sums_tiles[g][:, 0, :, :], func=ACT.Exp, scale=-1.0
-            )
-
-        def finish(g):
-            nc.vector.tensor_mul(
-                out=sums_tiles[g][:, 1, :, :], in0=sums_tiles[g][:, 1, :, :], in1=sums_tiles[g][:, 0, :, :]
-            )
-            store(GROUPS[g][0], GROUPS[g][1], sums_tiles[g][:, 1, :, :])
-
-        scalar_extra = [[] for t in range(STEPS + 1)]
-        vector_extra = [[] for t in range(STEPS + 1)]
-        for g in range(len(FIRST_LN)):
-            scalar_extra[LN_STEP].append((ln, g))
-            scalar_extra[LN_STEP + PAUSE + g].append((exp_of_minus, g))
-            vector_extra[LN_STEP + PAUSE + 1 + g].append((finish, g))
-        for g in range(len(FIRST_LN), len(GROUPS)):
-            scalar_extra[STEPS - 1].append((ln, g))
-        for g in range(len(FIRST_LN), len(GROUPS)):
-            scalar_extra[STEPS - 1].append((exp_of_minus, g))
-            vector_extra[STEPS].append((finish, g))
-
         def on(s):
-            return s is not None and 0 <= s < SLABS
+            return 0 <= s < SLABS
 
+        banks = {"xt_ps": x_banks, "h_ps": h_banks, "a_ps": a_banks, "sums_ps": sum_banks}
+        turn = ("xt_ps", "xt_ps", "h_ps", "h_ps", "a_ps", "a_ps", "sums_ps", "sums_ps")
+        pairs = list(range(EARLY, SLABS, 2))
+        products = [s for s in range(SLABS) if left_for_the_end(s)]
+
+        def sum_pair(k):
+            name = turn[k % len(turn)]
+            n_ps = banks[name].tile([P, PACK, P], F32, name=name)
+            live["n_ps", pairs[k]] = n_ps
+            for j in range(2):
+                for i in range(HALVES):
+                    add_up(n_ps[:, HALVES * j + i, :], live["xe", pairs[k] + j], i)
+
+        def finish_pair(k):
+            s = pairs[k]
+            part = s_all[:, blocks(s, s + 2), :]
+            nc.vector.tensor_mul(out=part, in0=live["n_ps", s][:], in1=part)
+            store(s, s + 2, part)
+
+        summed = 0
         transpose_x(0)
-        for t in range(STEPS + 1):
+        for t in range(SLABS + LEAD + 4):
+            if t + AHEAD < SLABS:
+                load_x(t + AHEAD)
             f = t
-            b = back_slab(t)
-            c = [None if b is None else b - k for k in range(4)]
-            relu_all = t >= LN_STEP
+            b = t - LEAD
+            has_product = on(b - 3) and not left_for_the_end(b - 3)
+            relu_all = t < 2 or not has_product
+            relu_halves = (0, 1) if relu_all else (0,)
             if on(f - 1):
                 first_matmul(f - 1)
-            if on(c[0]):
-                second_matmul(c[0])
+            if on(b):
+                second_matmul(b)
             if on(f + 1):
                 transpose_x(f + 1)
+            if on(b - 2):
+                sum_e(b - 2)
             if t == 0:
                 quantise_weights(w1_codes, w1_scales, w1_grouped)
             if on(f):
                 copy_x(f)
-            if on(c[2]):
-                multiply_by_x(c[2])
-                sums(c[2])
+            if has_product:
+                multiply_by_x(b - 3)
+                if b - 3 < EARLY:
+                    sum_xe(b - 3)
             if on(f - 1):
-                relu_on_vector(f - 1, (0, 1) if relu_all else (0,))
+                relu_on_vector(f - 1, relu_halves)
             if on(f):
                 quantise_x(f)
             if t == 1:
                 quantise_weights(w2_codes, w2_scales, w2_grouped)
-            for work, g in scalar_extra[t]:
-                work(g)
-            if on(c[1]):
-                exp(c[1])
-            if on(f - 1) and not relu_all:
-                relu_on_scalar(f - 1, 1)
-            for work, g in vector_extra[t]:
-                work(g)
+            if on(b - 1):
+                exp(b - 1)
+            if on(f - 1):
+                for i in range(len(relu_halves), HALVES):
+                    relu_on_scalar(f - 1, i)
             if on(f - 1):
                 quantise_h(f - 1)
-            if on(c[0]):
-                tanh(c[0])
-            if on(c[3]):
-                sums_out(c[3])
+            if on(b):
+                tanh(b)
+            for s in [] if t <= SLABS else products[:2]:
+                multiply_by_x(s)
+                products.remove(s)
+            while t > SLABS + 1 and summed < min(len(turn), 2 * (t - SLABS - 1)) and ("xe", pairs[summed] + 1) in live:
+                sum_pair(summed)
+                summed += 1
+            if on(b - 3):
+                s_out(b - 3, not has_product)
+            if 0 <= b - 4 < EARLY:
+                n_out(b - 4)
+
+        groups = [(s, s + LN_SLABS) for s in range(0, SLABS, LN_SLABS)]
+        for s0, s1 in groups:
+            part = s_all[:, blocks(s0, s1), :]
+            nc.scalar.activation(out=part, in_=part, func=ACT.Ln)
+        for s0, s1 in groups:
+            part = s_all[:, blocks(s0, s1), :]
+            nc.scalar.activation(out=part, in_=part, func=ACT.Exp, scale=-1.0)
+        while summed < min(len(turn), len(pairs)):
+            for s in pairs[summed], pairs[summed] + 1:
+                if ("xe", s) not in live:
+                    multiply_by_x(s)
+                    products.remove(s)
+            sum_pair(summed)
+            summed += 1
+        for s in products:
+            multiply_by_x(s)
+        if EARLY:
+            early = slice(0, HALVES * EARLY)
+            nc.vector.tensor_mul(out=n_early[:], in0=n_early[:], in1=s_all[:, early, :])
+            store(0, EARLY, n_early[:])
+        for k in range(len(pairs)):
+            finish_pair(k)
+            if k + len(turn) < len(pairs):
+                sum_pair(k + len(turn))

@@ -41,10 +41,10 @@ def tile_dwamformer_pa_t_kernel(tc, x, w1, w2, out):
         mx_pool = ctx.enter_context(tc.tile_pool(name="mx_pool", bufs=4))
         h_pool = ctx.enter_context(tc.tile_pool(name="h_pool", bufs=3))
         x_pool = ctx.enter_context(tc.tile_pool(name="x_pool", bufs=8))
-        x_banks = ctx.enter_context(tc.psum_pool(name="x_banks", bufs=2))
+        x_banks = ctx.enter_context(tc.psum_pool(name="x_banks", bufs=1))
         h_banks = ctx.enter_context(tc.psum_pool(name="h_banks", bufs=2))
         a_banks = ctx.enter_context(tc.psum_pool(name="a_banks", bufs=2))
-        sum_banks = ctx.enter_context(tc.psum_pool(name="sum_banks", bufs=2))
+        sum_banks = ctx.enter_context(tc.psum_pool(name="sum_banks", bufs=3))
         ctx.enter_context(tc.manual_schedule())
 
         ident_bf16 = keep.tile([P, P], BF16)
@@ -253,7 +253,7 @@ def tile_dwamformer_pa_t_kernel(tc, x, w1, w2, out):
             return 0 <= s < SLABS
 
         banks = {"xt_ps": x_banks, "h_ps": h_banks, "a_ps": a_banks, "sums_ps": sum_banks}
-        turn = ("xt_ps", "xt_ps", "h_ps", "h_ps", "a_ps", "a_ps", "sums_ps", "sums_ps")
+        turn = ("h_ps", "h_ps", "a_ps", "a_ps", "sums_ps", "sums_ps", "sums_ps")
         pairs = list(range(EARLY, SLABS, 2))
         products = [s for s in range(SLABS) if left_for_the_end(s)]
 
@@ -270,6 +270,19 @@ def tile_dwamformer_pa_t_kernel(tc, x, w1, w2, out):
             part = s_all[:, blocks(s, s + 2), :]
             nc.vector.tensor_mul(out=part, in0=live["n_ps", s][:], in1=part)
             store(s, s + 2, part)
+
+        def keep_warm(n):
+            idle_ps = x_banks.tile([P, 512], F32, name="xt_ps")
+            for i in range(n):
+                nc.tensor.matmul_mx(
+                    out=idle_ps[:],
+                    lhsT=w1_codes[:, 0:P].bitcast(FP8X4),
+                    lhsT_scale=w1_scales[:, 0:P],
+                    rhs=w1_codes[:].bitcast(FP8X4),
+                    rhs_scale=w1_scales[:],
+                    start=True,
+                    stop=True,
+                )
 
         summed = 0
         transpose_x(0)
@@ -289,10 +302,12 @@ def tile_dwamformer_pa_t_kernel(tc, x, w1, w2, out):
                 transpose_x(f + 1)
             if on(b - 2):
                 sum_e(b - 2)
-            if t == 0:
-                quantise_weights(w1_codes, w1_scales, w1_grouped)
+            if t in (34, 35):
+                keep_warm(4)
             if on(f):
                 copy_x(f)
+            if t == 0:
+                quantise_weights(w1_codes, w1_scales, w1_grouped)
             if has_product:
                 multiply_by_x(b - 3)
                 if b - 3 < EARLY:
@@ -337,6 +352,7 @@ def tile_dwamformer_pa_t_kernel(tc, x, w1, w2, out):
                     products.remove(s)
             sum_pair(summed)
             summed += 1
+        keep_warm(14)
         for s in products:
             multiply_by_x(s)
         if EARLY:

@@ -18,12 +18,13 @@ SLABS = 32
 WIN = 256
 FRAMES = WIN * PACK
 HALVES = WIN // P
-BY_PRODUCT = 6
+BY_PRODUCT = 5
 
 LEAD = 2
 EARLY = 4
 AHEAD = 6
 LN_SLABS = 4
+EARLY_AFTER = 16
 
 
 def left_for_the_end(s):
@@ -52,21 +53,35 @@ def tile_dwamformer_pa_t_kernel(tc, x, w1, w2, out):
         ident_f32 = keep.tile([P, P], F32)
         make_identity(nc, ident_f32[:])
 
+        nothing = keep.tile([P, 512], BF16)
+        nc.vector.memset(nothing[:], 0.0)
+        idle_ps = h_banks.tile([P, PACK, P], F32, name="h_ps")
+        for i in range(8):
+            nc.tensor.matmul(
+                out=idle_ps[:].rearrange("p t r -> p (t r)"),
+                lhsT=ident_bf16[:],
+                rhs=nothing[:],
+                start=True,
+                stop=True,
+            )
+
         x_tiles = {}
 
         def load_x(s):
             x_sb = x_pool.tile([P, FRAMES // P, P], BF16)
             x_tiles[s] = x_sb
-            for j in range(FRAMES // P):
-                first = s * FRAMES + j * P
-                nc.sync.dma_start(out=x_tiles[s][:, j, :], in_=frames[first : first + P, :])
+            nc.sync.dma_start(
+                out=x_tiles[s][:],
+                in_=frames[s * FRAMES : (s + 1) * FRAMES, :].rearrange("(j p) c -> p j c", p=P),
+            )
 
         w1_rows = keep.tile([P, PACK, 512], BF16, name="e_28", align_bytes=64)
         w2_rows = keep.tile([P, PACK, 512], BF16, name="e_29", align_bytes=64)
         nc.sync.dma_start(out=w1_rows[:], in_=w1.rearrange("(p j) f -> p j f", j=PACK))
         load_x(0)
+        load_x(1)
         nc.sync.dma_start(out=w2_rows[:], in_=w2.rearrange("(p j) f -> p j f", j=PACK))
-        for s in range(1, AHEAD):
+        for s in range(2, AHEAD):
             load_x(s)
 
         w1_grouped = keep.tile([P, PACK, P, PACK], BF16, name="e_30", align_bytes=64)
@@ -112,7 +127,10 @@ def tile_dwamformer_pa_t_kernel(tc, x, w1, w2, out):
                 xt = keep.tile([P, FRAMES], BF16, name="xt_%d" % s, align_bytes=64)
             else:
                 xt = xt_pool.tile([P, FRAMES], BF16, align_bytes=64)
-            nc.vector.tensor_copy(out=xt[:], in_=live["xt_ps", s][:])
+            nc.vector.tensor_copy(
+                out=xt[:].rearrange("p (i r m) -> p i r m", i=HALVES, m=PACK),
+                in_=live["xt_ps", s][:].rearrange("p (r i m) -> p i r m", i=HALVES, m=PACK),
+            )
             live["xt", s] = xt
 
         def quantise_x(s):
@@ -246,7 +264,8 @@ def tile_dwamformer_pa_t_kernel(tc, x, w1, w2, out):
 
         def store(s0, s1, result):
             nc.sync.dma_start(
-                out=rows[s0 * WIN : s1 * WIN, :].rearrange("(n p) c -> p n c", p=P), in_=result
+                out=rows[s0 * WIN : s1 * WIN, :].rearrange("(s p i) c -> p s (i c)", p=P, i=HALVES),
+                in_=result.rearrange("p (s i) c -> p s (i c)", i=HALVES),
             )
 
         def on(s):
@@ -257,8 +276,15 @@ def tile_dwamformer_pa_t_kernel(tc, x, w1, w2, out):
         pairs = list(range(EARLY, SLABS, 2))
         products = [s for s in range(SLABS) if left_for_the_end(s)]
 
-        def sum_pair(k):
-            name = turn[k % len(turn)]
+        def ln(s0, s1):
+            part = s_all[:, blocks(s0, s1), :]
+            nc.scalar.activation(out=part, in_=part, func=ACT.Ln)
+
+        def exp_of_minus(s0, s1):
+            part = s_all[:, blocks(s0, s1), :]
+            nc.scalar.activation(out=part, in_=part, func=ACT.Exp, scale=-1.0)
+
+        def sum_pair(k, name):
             n_ps = banks[name].tile([P, PACK, P], F32, name=name)
             live["n_ps", pairs[k]] = n_ps
             for j in range(2):
@@ -304,10 +330,10 @@ def tile_dwamformer_pa_t_kernel(tc, x, w1, w2, out):
                 sum_e(b - 2)
             if t in (34, 35):
                 keep_warm(4)
-            if on(f):
-                copy_x(f)
             if t == 0:
                 quantise_weights(w1_codes, w1_scales, w1_grouped)
+            if on(f):
+                copy_x(f)
             if has_product:
                 multiply_by_x(b - 3)
                 if b - 3 < EARLY:
@@ -331,35 +357,39 @@ def tile_dwamformer_pa_t_kernel(tc, x, w1, w2, out):
                 multiply_by_x(s)
                 products.remove(s)
             while t > SLABS + 1 and summed < min(len(turn), 2 * (t - SLABS - 1)) and ("xe", pairs[summed] + 1) in live:
-                sum_pair(summed)
+                sum_pair(summed, turn[summed])
                 summed += 1
             if on(b - 3):
                 s_out(b - 3, not has_product)
             if 0 <= b - 4 < EARLY:
                 n_out(b - 4)
 
-        groups = [(s, s + LN_SLABS) for s in range(0, SLABS, LN_SLABS)]
-        for s0, s1 in groups:
-            part = s_all[:, blocks(s0, s1), :]
-            nc.scalar.activation(out=part, in_=part, func=ACT.Ln)
-        for s0, s1 in groups:
-            part = s_all[:, blocks(s0, s1), :]
-            nc.scalar.activation(out=part, in_=part, func=ACT.Exp, scale=-1.0)
-        while summed < min(len(turn), len(pairs)):
+        for s0 in range(0, SLABS, LN_SLABS):
+            ln(s0, s0 + LN_SLABS)
+        for s0 in range(EARLY, EARLY + LN_SLABS, 2):
+            exp_of_minus(s0, s0 + 2)
+        for s0 in range(EARLY + LN_SLABS, SLABS, LN_SLABS):
+            exp_of_minus(s0, s0 + LN_SLABS)
+            if s0 == EARLY_AFTER:
+                exp_of_minus(0, EARLY)
+        while summed < len(turn):
             for s in pairs[summed], pairs[summed] + 1:
                 if ("xe", s) not in live:
                     multiply_by_x(s)
                     products.remove(s)
-            sum_pair(summed)
+            sum_pair(summed, turn[summed])
             summed += 1
-        keep_warm(14)
+        keep_warm(5)
         for s in products:
             multiply_by_x(s)
-        if EARLY:
-            early = slice(0, HALVES * EARLY)
-            nc.vector.tensor_mul(out=n_early[:], in0=n_early[:], in1=s_all[:, early, :])
-            store(0, EARLY, n_early[:])
+        sum_pair(summed, "xt_ps")
+        summed += 1
         for k in range(len(pairs)):
             finish_pair(k)
-            if k + len(turn) < len(pairs):
-                sum_pair(k + len(turn))
+            if summed < len(pairs):
+                sum_pair(summed, (turn + ("xt_ps",))[k])
+                summed += 1
+            if pairs[k] + 2 == EARLY_AFTER + LN_SLABS:
+                early = slice(0, HALVES * EARLY)
+                nc.vector.tensor_mul(out=n_early[:], in0=n_early[:], in1=s_all[:, early, :])
+                store(0, EARLY, n_early[:])

@@ -28,7 +28,7 @@ EARLY_AFTER = 16
 
 
 def left_for_the_end(s):
-    return s >= 4 and s % 2 == 1
+    return s >= 4 and (s % 2 == 1 or s % 8 == 0)
 
 
 def tile_dwamformer_pa_t_kernel(tc, x, w1, w2, out):
@@ -212,8 +212,30 @@ def tile_dwamformer_pa_t_kernel(tc, x, w1, w2, out):
             e = live["e", s]
             nc.scalar.activation(out=e[:], in_=e[:], func=ACT.Exp, scale=0.5)
 
+        gpsimd_done = {}
+
+        def multiply_on_gpsimd(s):
+            e = live["e", s]
+            nc.gpsimd.tensor_tensor(
+                out=e[:, 0:2, :],
+                in0=e[:, 0:2, :],
+                in1=live["xt", s][:].rearrange("p (r m) -> p m r", m=PACK)[:, 0:2, :],
+                op=mybir.AluOpType.mult,
+            )
+            gpsimd_done[s] = 2
+
         def multiply_by_x(s):
             e = live["e", s]
+            first = gpsimd_done.get(s, 0)
+            if first:
+                nc.vector.tensor_tensor(
+                    out=e[:, first:, :],
+                    in0=e[:, first:, :],
+                    in1=live["xt", s][:].rearrange("p (r m) -> p m r", m=PACK)[:, first:, :],
+                    op=mybir.AluOpType.mult,
+                )
+                live["xe", s] = e
+                return
             if s < EARLY:
                 xe = keep.tile([P, PACK, WIN], F32, name="e_%d" % (s + 2 * EARLY), align_bytes=64)
             else:
@@ -334,6 +356,8 @@ def tile_dwamformer_pa_t_kernel(tc, x, w1, w2, out):
                 quantise_weights(w1_codes, w1_scales, w1_grouped)
             if on(f):
                 copy_x(f)
+            if on(b - 3) and left_for_the_end(b - 3) and True:
+                multiply_on_gpsimd(b - 3)
             if has_product:
                 multiply_by_x(b - 3)
                 if b - 3 < EARLY:
@@ -360,7 +384,7 @@ def tile_dwamformer_pa_t_kernel(tc, x, w1, w2, out):
                 sum_pair(summed, turn[summed])
                 summed += 1
             if on(b - 3):
-                s_out(b - 3, not has_product)
+                s_out(b - 3, not has_product or t > SLABS)
             if 0 <= b - 4 < EARLY:
                 n_out(b - 4)
 

from contextlib import ExitStack

import concourse.mybir as mybir
from concourse.masks import make_identity

FLOPS = 2 * 2 * 8192 * 512 * 512

BF16 = mybir.dt.bfloat16
F32 = mybir.dt.float32
U32 = mybir.dt.uint32
U8 = mybir.dt.uint8
FP8X4 = mybir.dt.float8_e4m3fn_x4
ACT = mybir.ActivationFunctionType

P = 128
PACK = 4
SLABS = 32
WIN = 256
FRAMES = WIN * PACK
HALVES = WIN // P
BY_PRODUCT = 5

LEAD = 2
EARLY = 4
AHEAD = 6
LN_SLABS = 4
EARLY_AFTER = 16


def left_for_the_end(s):
    return s >= 4 and (s % 2 == 1 or s % 8 == 0)


def tile_dwamformer_pa_t_kernel(tc, x, w1, w2, out):
    nc = tc.nc
    frames = x.flatten_outer_dims()
    rows = out.flatten_outer_dims()

    with ExitStack() as ctx:
        keep = ctx.enter_context(tc.tile_pool(name="keep", bufs=1))
        xt_pool = ctx.enter_context(tc.tile_pool(name="xt_pool", bufs=6))
        mx_pool = ctx.enter_context(tc.tile_pool(name="mx_pool", bufs=4))
        h_pool = ctx.enter_context(tc.tile_pool(name="h_pool", bufs=3))
        x_pool = ctx.enter_context(tc.tile_pool(name="x_pool", bufs=8))
        x_banks = ctx.enter_context(tc.psum_pool(name="x_banks", bufs=1))
        h_banks = ctx.enter_context(tc.psum_pool(name="h_banks", bufs=2))
        a_banks = ctx.enter_context(tc.psum_pool(name="a_banks", bufs=2))
        sum_banks = ctx.enter_context(tc.psum_pool(name="sum_banks", bufs=3))
        ctx.enter_context(tc.manual_schedule())

        ident_bf16 = keep.tile([P, P], BF16)
        make_identity(nc, ident_bf16[:])
        ident_f32 = keep.tile([P, P], F32)
        make_identity(nc, ident_f32[:])

        nothing = keep.tile([P, 512], BF16)
        nc.vector.memset(nothing[:], 0.0)
        idle_ps = h_banks.tile([P, PACK, P], F32, name="h_ps")
        for i in range(8):
            nc.tensor.matmul(
                out=idle_ps[:].rearrange("p t r -> p (t r)"),
                lhsT=ident_bf16[:],
                rhs=nothing[:],
                start=True,
                stop=True,
            )

        x_tiles = {}

        def load_x(s):
            x_sb = x_pool.tile([P, FRAMES // P, P], BF16)
            x_tiles[s] = x_sb
            nc.sync.dma_start(
                out=x_tiles[s][:],
                in_=frames[s * FRAMES : (s + 1) * FRAMES, :].rearrange("(j p) c -> p j c", p=P),
            )

        w1_rows = keep.tile([P, PACK, 512], BF16, name="e_28", align_bytes=64)
        w2_rows = keep.tile([P, PACK, 512], BF16, name="e_29", align_bytes=64)
        nc.sync.dma_start(out=w1_rows[:], in_=w1.rearrange("(p j) f -> p j f", j=PACK))
        load_x(0)
        load_x(1)
        nc.sync.dma_start(out=w2_rows[:], in_=w2.rearrange("(p j) f -> p j f", j=PACK))
        for s in range(2, AHEAD):
            load_x(s)

        w1_grouped = keep.tile([P, PACK, P, PACK], BF16, name="e_30", align_bytes=64)
        w2_grouped = keep.tile([P, PACK, P, PACK], BF16, name="e_31", align_bytes=64)
        w1_codes = keep.tile([P, 512], U32, align_bytes=64)
        w1_scales = keep.tile([P, 512], U8, align_bytes=64)
        w2_codes = keep.tile([P, 512], U32, align_bytes=64)
        w2_scales = keep.tile([P, 512], U8, align_bytes=64)
        w1_view = w1_rows[:].rearrange("p j (q t) -> p t q j", t=PACK)
        nc.vector.tensor_copy(out=w1_grouped[:, 0:2, :, :], in_=w1_view[:, 0:2, :, :])
        nc.scalar.copy(out=w1_grouped[:, 2:4, :, :], in_=w1_view[:, 2:4, :, :])
        nc.scalar.copy(out=w2_grouped[:], in_=w2_rows[:].rearrange("p j (q t) -> p t q j", t=PACK))

        def quantise_weights(codes, scales, grouped):
            nc.vector.quantize_mx(
                out=codes[:].bitcast(FP8X4),
                scales=scales[:],
                in_=grouped[:].rearrange("p t q j -> p (t q j)"),
            )

        s_all = keep.tile([P, SLABS * HALVES, P], F32)
        n_early = keep.tile([P, EARLY * HALVES, P], F32)

        live = {}

        def transpose_x(s):
            xt_ps = x_banks.tile([P, FRAMES], BF16, name="xt_ps")
            for j in range(FRAMES // P):
                if j < BY_PRODUCT:
                    nc.tensor.matmul(
                        out=xt_ps[:, j * P : (j + 1) * P],
                        lhsT=x_tiles[s][:, j, :],
                        rhs=ident_bf16[:],
                        start=True,
                        stop=True,
                    )
                else:
                    nc.tensor.transpose(xt_ps[:, j * P : (j + 1) * P], x_tiles[s][:, j, :], ident_bf16[:])
            live["xt_ps", s] = xt_ps

        def copy_x(s):
            if left_for_the_end(s):
                xt = keep.tile([P, FRAMES], BF16, name="xt_%d" % s, align_bytes=64)
            else:
                xt = xt_pool.tile([P, FRAMES], BF16, align_bytes=64)
            nc.vector.tensor_copy(
                out=xt[:].rearrange("p (i r m) -> p i r m", i=HALVES, m=PACK),
                in_=live["xt_ps", s][:].rearrange("p (r i m) -> p i r m", i=HALVES, m=PACK),
            )
            live["xt", s] = xt

        def quantise_x(s):
            x_codes = mx_pool.tile([P, WIN], U32, align_bytes=64)
            x_scales = mx_pool.tile([P, WIN], U8, align_bytes=64)
            nc.vector.quantize_mx(out=x_codes[:].bitcast(FP8X4), scales=x_scales[:], in_=live["xt", s][:])
            live["x_mx", s] = (x_codes, x_scales)

        def first_matmul(s):
            x_codes, x_scales = live["x_mx", s]
            for i in range(HALVES):
                h_ps = h_banks.tile([P, PACK, P], F32, name="h_ps")
                for t in range(PACK):
                    nc.tensor.matmul_mx(
                        out=h_ps[:, t, :],
                        lhsT=w1_codes[:, t * P : (t + 1) * P].bitcast(FP8X4),
                        lhsT_scale=w1_scales[:, t * P : (t + 1) * P],
                        rhs=x_codes[:, i * P : (i + 1) * P].bitcast(FP8X4),
                        rhs_scale=x_scales[:, i * P : (i + 1) * P],
                        start=True,
                        stop=True,
                    )
                live["h_ps", s, i] = h_ps

        def relu_on_vector(s, halves):
            if ("h", s) not in live:
                h_bf16 = h_pool.tile([P, WIN, PACK], BF16, align_bytes=64)
                live["h", s] = h_bf16
            for i in halves:
                nc.vector.tensor_scalar_max(
                    out=live["h", s][:, i * P : (i + 1) * P, :],
                    in0=live["h_ps", s, i][:].rearrange("p t r -> p r t"),
                    scalar1=0.0,
                )

        def relu_on_scalar(s, i):
            nc.scalar.activation(
                out=live["h", s][:, i * P : (i + 1) * P, :],
                in_=live["h_ps", s, i][:].rearrange("p t r -> p r t"),
                func=ACT.Relu,
            )

        def quantise_h(s):
            h_codes = mx_pool.tile([P, WIN], U32, align_bytes=64)
            h_scales = mx_pool.tile([P, WIN], U8, align_bytes=64)
            nc.vector.quantize_mx(
                out=h_codes[:].bitcast(FP8X4),
                scales=h_scales[:],
                in_=live["h", s][:].rearrange("p r t -> p (r t)"),
            )
            live["h_mx", s] = (h_codes, h_scales)

        def second_matmul(s):
            h_codes, h_scales = live["h_mx", s]
            for u in range(2):
                a_ps = a_banks.tile([P, 2, WIN], F32, name="a_ps")
                for v in range(2):
                    m = 2 * u + v
                    nc.tensor.matmul_mx(
                        out=a_ps[:, v, :],
                        lhsT=w2_codes[:, m * P : (m + 1) * P].bitcast(FP8X4),
                        lhsT_scale=w2_scales[:, m * P : (m + 1) * P],
                        rhs=h_codes[:].bitcast(FP8X4),
                        rhs_scale=h_scales[:],
                        start=True,
                        stop=True,
                    )
                live["a_ps", s, u] = a_ps

        def tanh(s):
            e = keep.tile([P, PACK, WIN], F32, name="e_%d" % (s if s >= EARLY else s + EARLY), align_bytes=64)
            for u in range(2):
                nc.scalar.activation(
                    out=e[:, 2 * u : 2 * u + 2, :], in_=live["a_ps", s, u][:], func=ACT.Tanh, scale=0.5
                )
            live["e", s] = e

        def exp(s):
            e = live["e", s]
            nc.scalar.activation(out=e[:], in_=e[:], func=ACT.Exp, scale=0.5)

        gpsimd_done = {}

        def multiply_on_gpsimd(s):
            e = live["e", s]
            nc.gpsimd.tensor_tensor(
                out=e[:, 0:2, :],
                in0=e[:, 0:2, :],
                in1=live["xt", s][:].rearrange("p (r m) -> p m r", m=PACK)[:, 0:2, :],
                op=mybir.AluOpType.mult,
            )
            gpsimd_done[s] = 2

        def multiply_by_x(s):
            e = live["e", s]
            first = gpsimd_done.get(s, 0)
            if first:
                nc.vector.tensor_tensor(
                    out=e[:, first:, :],
                    in0=e[:, first:, :],
                    in1=live["xt", s][:].rearrange("p (r m) -> p m r", m=PACK)[:, first:, :],
                    op=mybir.AluOpType.mult,
                )
                live["xe", s] = e
                return
            if s < EARLY:
                xe = keep.tile([P, PACK, WIN], F32, name="e_%d" % (s + 2 * EARLY), align_bytes=64)
            else:
                xe = e
            nc.vector.tensor_tensor(
                out=xe[:],
                in0=e[:],
                in1=live["xt", s][:].rearrange("p (r m) -> p m r", m=PACK),
                op=mybir.AluOpType.mult,
            )
            live["xe", s] = xe

        def add_up(dst, tile, i):
            for m in range(PACK):
                nc.tensor.matmul(
                    out=dst,
                    lhsT=tile[:, m, i * P : (i + 1) * P],
                    rhs=ident_f32[:],
                    is_transpose=True,
                    start=(m == 0),
                    stop=(m == PACK - 1),
                )

        def sum_e(s):
            sums_ps = sum_banks.tile([P, PACK, P], F32, name="sums_ps")
            live["s_ps", s] = sums_ps
            for i in range(HALVES):
                add_up(sums_ps[:, i, :], live["e", s], i)

        def sum_xe(s):
            sums_ps = sum_banks.tile([P, PACK, P], F32, name="sums_ps")
            live["n_ps", s] = sums_ps
            for i in range(HALVES):
                add_up(sums_ps[:, i, :], live["xe", s], i)

        def blocks(s0, s1):
            return slice(HALVES * s0, HALVES * s1)

        def s_out(s, on_vector):
            dst, src = s_all[:, blocks(s, s + 1), :], live["s_ps", s][:, 0:HALVES, :]
            if on_vector:
                nc.vector.tensor_copy(out=dst, in_=src)
            else:
                nc.scalar.copy(out=dst, in_=src)

        def n_out(s):
            nc.scalar.copy(out=n_early[:, blocks(s, s + 1), :], in_=live["n_ps", s][:, 0:HALVES, :])

        def store(s0, s1, result):
            nc.sync.dma_start(
                out=rows[s0 * WIN : s1 * WIN, :].rearrange("(s p i) c -> p s (i c)", p=P, i=HALVES),
                in_=result.rearrange("p (s i) c -> p s (i c)", i=HALVES),
            )

        def on(s):
            return 0 <= s < SLABS

        banks = {"xt_ps": x_banks, "h_ps": h_banks, "a_ps": a_banks, "sums_ps": sum_banks}
        turn = ("h_ps", "h_ps", "a_ps", "a_ps", "sums_ps", "sums_ps", "sums_ps")
        pairs = list(range(EARLY, SLABS, 2))
        products = [s for s in range(SLABS) if left_for_the_end(s)]

        def ln(s0, s1):
            part = s_all[:, blocks(s0, s1), :]
            nc.scalar.activation(out=part, in_=part, func=ACT.Ln)

        def exp_of_minus(s0, s1):
            part = s_all[:, blocks(s0, s1), :]
            nc.scalar.activation(out=part, in_=part, func=ACT.Exp, scale=-1.0)

        def sum_pair(k, name):
            n_ps = banks[name].tile([P, PACK, P], F32, name=name)
            live["n_ps", pairs[k]] = n_ps
            for j in range(2):
                for i in range(HALVES):
                    add_up(n_ps[:, HALVES * j + i, :], live["xe", pairs[k] + j], i)

        def finish_pair(k):
            s = pairs[k]
            part = s_all[:, blocks(s, s + 2), :]
            nc.vector.tensor_mul(out=part, in0=live["n_ps", s][:], in1=part)
            store(s, s + 2, part)

        def keep_warm(n):
            idle_ps = x_banks.tile([P, 512], F32, name="xt_ps")
            for i in range(n):
                nc.tensor.matmul_mx(
                    out=idle_ps[:],
                    lhsT=w1_codes[:, 0:P].bitcast(FP8X4),
                    lhsT_scale=w1_scales[:, 0:P],
                    rhs=w1_codes[:].bitcast(FP8X4),
                    rhs_scale=w1_scales[:],
                    start=True,
                    stop=True,
                )

        summed = 0
        transpose_x(0)
        for t in range(SLABS + LEAD + 4):
            if t + AHEAD < SLABS:
                load_x(t + AHEAD)
            f = t
            b = t - LEAD
            has_product = on(b - 3) and not left_for_the_end(b - 3)
            relu_all = t < 2 or not has_product
            relu_halves = (0, 1) if relu_all else (0,)
            if on(f - 1):
                first_matmul(f - 1)
            if on(b):
                second_matmul(b)
            if on(f + 1):
                transpose_x(f + 1)
            if on(b - 2):
                sum_e(b - 2)
            if t in (34, 35):
                keep_warm(4)
            if t == 0:
                quantise_weights(w1_codes, w1_scales, w1_grouped)
            if on(f):
                copy_x(f)
            if on(b - 3) and left_for_the_end(b - 3) and True:
                multiply_on_gpsimd(b - 3)
            if has_product:
                multiply_by_x(b - 3)
                if b - 3 < EARLY:
                    sum_xe(b - 3)
            if on(f - 1):
                relu_on_vector(f - 1, relu_halves)
            if on(f):
                quantise_x(f)
            if t == 1:
                quantise_weights(w2_codes, w2_scales, w2_grouped)
            if on(b - 1):
                exp(b - 1)
            if on(f - 1):
                for i in range(len(relu_halves), HALVES):
                    relu_on_scalar(f - 1, i)
            if on(f - 1):
                quantise_h(f - 1)
            if on(b):
                tanh(b)
            for s in [] if t <= SLABS else products[:2]:
                multiply_by_x(s)
                products.remove(s)
            while t > SLABS + 1 and summed < min(len(turn), 2 * (t - SLABS - 1)) and ("xe", pairs[summed] + 1) in live:
                sum_pair(summed, turn[summed])
                summed += 1
            if on(b - 3):
                s_out(b - 3, not has_product or t > SLABS)
            if 0 <= b - 4 < EARLY:
                n_out(b - 4)

        for s0 in range(0, SLABS, LN_SLABS):
            ln(s0, s0 + LN_SLABS)
        for s0 in range(EARLY, EARLY + LN_SLABS, 2):
            exp_of_minus(s0, s0 + 2)
        for s0 in range(EARLY + LN_SLABS, SLABS, LN_SLABS):
            exp_of_minus(s0, s0 + LN_SLABS)
            if s0 == EARLY_AFTER:
                exp_of_minus(0, EARLY)
        while summed < len(turn):
            for s in pairs[summed], pairs[summed] + 1:
                if ("xe", s) not in live:
                    multiply_by_x(s)
                    products.remove(s)
            sum_pair(summed, turn[summed])
            summed += 1
        keep_warm(5)
        for s in products:
            multiply_by_x(s)
        sum_pair(summed, "xt_ps")
        summed += 1
        for k in range(len(pairs)):
            finish_pair(k)
            if summed < len(pairs):
                sum_pair(summed, (turn + ("xt_ps",))[k])
                summed += 1
            if pairs[k] + 2 == EARLY_AFTER + LN_SLABS:
                early = slice(0, HALVES * EARLY)
                nc.vector.tensor_mul(out=n_early[:], in0=n_early[:], in1=s_all[:, early, :])
                store(0, EARLY, n_early[:])
